import numpy as np
import ml_dtypes


def mxq(x, axis, fmt="e4m3"):
    dtype, down = {"e4m3": (ml_dtypes.float8_e4m3fn, 7), "e5m2": (ml_dtypes.float8_e5m2, 14)}[fmt]
    v = np.moveaxis(np.asarray(x, np.float32).astype(ml_dtypes.bfloat16).astype(np.float64), axis, -1)
    blocks = v.reshape(v.shape[:-1] + (-1, 32))
    amax = np.abs(blocks).max(-1, keepdims=True)
    byte = np.maximum(np.where(amax > 0, np.frexp(amax)[1] - 1 + 127, 0) - down, 1)
    scale = np.exp2(byte - 127.0)
    codes = (blocks / scale).astype(np.float32).astype(dtype).astype(np.float64)
    return np.moveaxis((codes * scale).reshape(v.shape), -1, axis)


WIDE = False


def mx_kscale(k):
    if not WIDE:
        return np.ones(k)
    levels = np.array([10, -10, 5, -5, 0])
    a = np.random.permutation(np.resize(levels, k // 512 * 4)).reshape(k // 512, 4)
    idx = np.arange(k)
    return np.exp2(a[idx // 512, idx % 128 // 32])


BF16 = ml_dtypes.bfloat16


def bf(x):
    return np.asarray(x, np.float32).astype(BF16)


def f64(x):
    return np.asarray(x).astype(np.float64)


B, T, N, H, G, GH = 32, 4, 8, 512, 9, 3


def sigmoid(v):
    return 1.0 / (1.0 + np.exp(-v))


def setup_inputs():
    s = mx_kscale(H)
    return {"h_new": bf(np.random.standard_normal((B, T, N, H)) * 0.35 * s),
            "c_new": bf(np.random.standard_normal((B, T, N, H)) * 0.8),
            "g_s": bf(np.random.standard_normal((B, T, H)) * s),
            "c_g_s": bf(np.random.standard_normal((B, T, H)) * 0.5),
            "Wg_s": bf(np.random.standard_normal((GH, T, H, H)) * 2.0 / np.sqrt(H) / s[:, None]),
            "Zg_s": bf(np.random.standard_normal((GH, T, H, H)) * 1.0 / np.sqrt(H) / s[:, None]),
            "bg_s": bf(np.random.standard_normal((GH, T, 1, H)) * 0.3)}


def reference(h_new, c_new, g_s, c_g_s, Wg_s, Zg_s, bg_s):
    c_new, c_g_s = f64(c_new), f64(c_g_s)
    hq = mxq(f64(h_new).transpose(1, 0, 2, 3).reshape(T, B * N, H), 2, "e4m3")
    preg = (hq @ mxq(f64(Wg_s), 2, "e4m3")) + f64(bg_s)
    preg = preg.reshape(GH, T, B, N, H).transpose(0, 2, 1, 3, 4)
    zs_part = mxq(f64(g_s).transpose(1, 0, 2), 2, "e4m3") @ mxq(f64(Zg_s), 2, "e4m3")
    zs_part = zs_part.transpose(0, 2, 1, 3)[:, :, :, None]
    f_s, gg_s, o_s = sigmoid(preg + zs_part)
    c_g_s_new = np.mean(f_s * c_new, axis=2) + np.mean(gg_s, axis=2) * c_g_s
    g_s_new = np.mean(o_s, axis=2) * np.tanh(c_g_s_new)
    return g_s_new, c_g_s_new

@@ -1,0 +1,202 @@
+from contextlib import ExitStack
+
+import concourse.mybir as mybir
+from concourse.masks import make_identity
+
+BF16 = mybir.dt.bfloat16
+F32 = mybir.dt.float32
+U32 = mybir.dt.uint32
+U8 = mybir.dt.uint8
+FP8X4 = mybir.dt.float8_e4m3fn_x4
+ACT = mybir.ActivationFunctionType
+ALU = mybir.AluOpType
+
+P = 128
+PACK = 4
+SEQS = 32
+FRAMES = 4
+BONES = 8
+FEATS = 512
+GATES = 3
+BLOCKS = FEATS // P
+COLS = BONES * SEQS
+HALF = 2
+
+FLOPS = 2 * GATES * FRAMES * FEATS * FEATS * (COLS + SEQS)
+
+
+def tile_st_hmr_pc_kernel(tc, h_new, c_new, g_s, c_g_s, Wg_s, Zg_s, bg_s, out_0, out_1):
+    nc = tc.nc
+    with ExitStack() as ctx:
+        const = ctx.enter_context(tc.tile_pool(name="const", bufs=1))
+        raw_pool = ctx.enter_context(tc.tile_pool(name="raw", bufs=1))
+        grouped_pool = ctx.enter_context(tc.tile_pool(name="grouped", bufs=4))
+        code_pool = ctx.enter_context(tc.tile_pool(name="codes", bufs=6))
+        sig_pool = ctx.enter_context(tc.tile_pool(name="sig", bufs=3))
+        fin_pool = ctx.enter_context(tc.tile_pool(name="fin", bufs=2))
+        turn_psum = ctx.enter_context(tc.psum_pool(name="turn", bufs=2))
+        acc_psum = ctx.enter_context(tc.psum_pool(name="acc", bufs=4))
+        red_psum = ctx.enter_context(tc.psum_pool(name="red", bufs=2))
+
+        g_sb = const.tile([P, FEATS], BF16)
+        nc.sync.dma_start(out=g_sb[:], in_=g_s.rearrange("b t k -> (b t) k"))
+        h_sb = const.tile([P, BONES * FEATS], BF16)
+        c_sb = const.tile([P, BONES, FEATS], BF16)
+        bias_rows = const.tile([P, P], BF16)
+        nc.vector.memset(bias_rows[:], 0.0)
+        cgs_sb = const.tile([P, FRAMES, P], BF16)
+
+        raw = {}
+        for t in range(FRAMES):
+            for g in range(GATES):
+                for kind, weights in enumerate((Wg_s, Zg_s)):
+                    raw[(t, g, kind)] = raw_pool.tile([P, PACK, FEATS], BF16, name="raw_%d_%d_%d" % (t, g, kind))
+                    nc.sync.dma_start(
+                        out=raw[(t, g, kind)][:], in_=weights[g, t].rearrange("(p j) w -> p j w", j=PACK)
+                    )
+                if t == 0 and g == 0:
+                    nc.sync.dma_start(out=h_sb[:], in_=h_new.rearrange("b t n k -> (b t) (n k)"))
+                    nc.sync.dma_start(
+                        out=bias_rows[0 : GATES * FRAMES * BLOCKS, :],
+                        in_=bg_s.rearrange("g t o (f c) -> (g t o f) c", c=P),
+                    )
+                    nc.sync.dma_start(out=c_sb[:], in_=c_new.rearrange("b t n k -> (b t) n k"))
+                    for f in range(BLOCKS):
+                        nc.sync.dma_start(
+                            out=cgs_sb[f * SEQS : (f + 1) * SEQS, :, :], in_=c_g_s[:, :, f * P : (f + 1) * P]
+                        )
+
+        ident_f32 = const.tile([P, P], F32)
+        make_identity(nc, ident_f32[:])
+        ident_bf16 = const.tile([P, P], BF16)
+        make_identity(nc, ident_bf16[:])
+
+        def quantise_matrix(key, on_scalar):
+            grouped = grouped_pool.tile([P, FEATS, PACK], BF16, align_bytes=64, name="grouped")
+            dst = grouped[:].rearrange("p (c i) j -> p c j i", i=4)
+            src = raw[key][:].rearrange("p j (c i) -> p c j i", i=4)
+            if on_scalar:
+                nc.scalar.copy(out=dst, in_=src)
+            else:
+                nc.vector.tensor_copy(out=dst, in_=src)
+            codes = code_pool.tile([P, FEATS], U32, align_bytes=64, name="codes")
+            scales = code_pool.tile([P, FEATS], U8, align_bytes=64, name="scales")
+            nc.vector.quantize_mx(
+                out=codes[:].bitcast(FP8X4), scales=scales[:], in_=grouped[:].rearrange("p w j -> p (w j)")
+            )
+            return codes, scales
+
+        g_words = g_sb[:].bitcast(F32).rearrange("p (q u) -> p u q", u=HALF)
+        g_turned = turn_psum.tile([P, HALF, P], F32, tag="turn")
+        for u in range(HALF):
+            nc.tensor.transpose(g_turned[:, u, :], g_words[:, u, :], ident_f32[:])
+        g_grouped = const.tile([P, FRAMES * COLS * PACK], BF16, align_bytes=64)
+        g_grouped_words = g_grouped[:].bitcast(F32).rearrange(
+            "p (t n b u) -> p t n b u", t=FRAMES, n=BONES, u=HALF
+        )
+        for t in range(FRAMES):
+            one_frame = g_turned[:].rearrange("p u (b t) -> p t b u", t=FRAMES)[:, t]
+            nc.scalar.copy(
+                out=g_grouped_words[:, t], in_=one_frame.unsqueeze(1).to_broadcast([P, BONES, SEQS, HALF])
+            )
+        g_codes = const.tile([P, FRAMES * COLS], U32, align_bytes=64)
+        g_scales = const.tile([P, FRAMES * COLS], U8, align_bytes=64)
+        nc.vector.quantize_mx(out=g_codes[:].bitcast(FP8X4), scales=g_scales[:], in_=g_grouped[:])
+
+        h_words = h_sb[:].bitcast(F32).rearrange("p (n q u) -> p n u q", n=BONES, u=HALF)
+        h_grouped = const.tile([P, FRAMES * COLS * PACK], BF16, align_bytes=64)
+        h_grouped_words = h_grouped[:].bitcast(F32).rearrange(
+            "p (t n b u) -> p t n b u", t=FRAMES, n=BONES, u=HALF
+        )
+        for n in range(BONES):
+            h_turned = turn_psum.tile([P, HALF, P], F32, tag="turn")
+            for u in range(HALF):
+                nc.tensor.transpose(h_turned[:, u, :], h_words[:, n, u, :], ident_f32[:])
+            nc.scalar.copy(
+                out=h_grouped_words[:, :, n], in_=h_turned[:].rearrange("p u (b t) -> p t b u", t=FRAMES)
+            )
+        h_codes = const.tile([P, FRAMES * COLS], U32, align_bytes=64)
+        h_scales = const.tile([P, FRAMES * COLS], U8, align_bytes=64)
+        nc.vector.quantize_mx(out=h_codes[:].bitcast(FP8X4), scales=h_scales[:], in_=h_grouped[:])
+
+        bias_turned = turn_psum.tile([P, P], BF16, tag="turn")
+        nc.tensor.transpose(bias_turned[:], bias_rows[:], ident_bf16[:])
+        bias_sb = const.tile([P, GATES * FRAMES * BLOCKS], F32)
+        nc.vector.tensor_copy(out=bias_sb[:], in_=bias_turned[:, 0 : GATES * FRAMES * BLOCKS])
+
+        c_turned_sb = const.tile([P, FRAMES, BONES, BLOCKS, SEQS], BF16)
+        for n in range(BONES):
+            c_turned = turn_psum.tile([P, BLOCKS, P], BF16, tag="turn")
+            for f in range(BLOCKS):
+                nc.tensor.transpose(c_turned[:, f, :], c_sb[:, n, f * P : (f + 1) * P], ident_bf16[:])
+            nc.scalar.copy(
+                out=c_turned_sb[:, :, n], in_=c_turned[:].rearrange("p f (b t) -> p t f b", t=FRAMES)
+            )
+
+        count = 0
+        for t in range(FRAMES):
+            frame_cols = slice(t * COLS, (t + 1) * COLS)
+            red = red_psum.tile([P, GATES, P], F32)
+            for g in range(GATES):
+                operands = []
+                for kind in range(2):
+                    operands.append(quantise_matrix((t, g, kind), on_scalar=(count % 3 == 1)))
+                    count += 1
+                moving = ((h_codes, h_scales), (g_codes, g_scales))
+                sig = sig_pool.tile([P, BONES, BLOCKS, SEQS], F32)
+                for pair in range(BLOCKS // 2):
+                    acc = acc_psum.tile([P, 2, COLS], F32)
+                    for i in range(2):
+                        block_cols = slice((2 * pair + i) * P, (2 * pair + i + 1) * P)
+                        for kind in range(2):
+                            nc.tensor.matmul_mx(
+                                out=acc[:, i, :],
+                                lhsT=operands[kind][0][:, block_cols].bitcast(FP8X4),
+                                lhsT_scale=operands[kind][1][:, block_cols],
+                                rhs=moving[kind][0][:, frame_cols].bitcast(FP8X4),
+                                rhs_scale=moving[kind][1][:, frame_cols],
+                                start=(kind == 0),
+                                stop=(kind == 1),
+                            )
+                    for i in range(2):
+                        f = 2 * pair + i
+                        bias_col = (g * FRAMES + t) * BLOCKS + f
+                        nc.scalar.activation(
+                            out=sig[:, :, f, :],
+                            in_=acc[:, i, :].rearrange("p (n b) -> p n b", b=SEQS),
+                            func=ACT.Sigmoid,
+                            bias=bias_sb[:, bias_col : bias_col + 1],
+                        )
+                if g == 0:
+                    flat = sig[:].rearrange("p n f b -> p (n f b)")
+                    nc.vector.tensor_mul(
+                        out=flat, in0=flat, in1=c_turned_sb[:, t].rearrange("p n f b -> p (n f b)")
+                    )
+                for n in range(BONES):
+                    nc.tensor.matmul(
+                        out=red[:, g, :],
+                        lhsT=sig[:, n].rearrange("p f b -> p (f b)"),
+                        rhs=ident_f32[:],
+                        is_transpose=True,
+                        start=(n == 0),
+                        stop=(n == BONES - 1),
+                    )
+
+            kept = fin_pool.tile([P, P], F32)
+            nc.vector.scalar_tensor_tensor(
+                out=kept[:], in0=red[:, 1, :], scalar=1.0 / BONES, in1=cgs_sb[:, t, :], op0=ALU.mult, op1=ALU.mult
+            )
+            cell = fin_pool.tile([P, P], F32)
+            nc.vector.scalar_tensor_tensor(
+                out=cell[:], in0=red[:, 0, :], scalar=1.0 / BONES, in1=kept[:], op0=ALU.mult, op1=ALU.add
+            )
+            squashed = fin_pool.tile([P, P], F32)
+            nc.scalar.activation(out=squashed[:], in_=cell[:], func=ACT.Tanh)
+            hidden = fin_pool.tile([P, P], F32)
+            nc.vector.scalar_tensor_tensor(
+                out=hidden[:], in0=red[:, 2, :], scalar=1.0 / BONES, in1=squashed[:], op0=ALU.mult, op1=ALU.mult
+            )
+            for f in range(BLOCKS):
+                rows = slice(f * SEQS, (f + 1) * SEQS)
+                nc.sync.dma_start(out=out_1[:, t, f * P : (f + 1) * P], in_=cell[rows, :])
+                nc.sync.dma_start(out=out_0[:, t, f * P : (f + 1) * P], in_=hidden[rows, :])

@@ -5,6 +5,7 @@ from concourse.masks import make_identity
 
 BF16 = mybir.dt.bfloat16
 F32 = mybir.dt.float32
+I32 = mybir.dt.int32
 U32 = mybir.dt.uint32
 U8 = mybir.dt.uint8
 FP8X4 = mybir.dt.float8_e4m3fn_x4
@@ -13,6 +14,7 @@ ALU = mybir.AluOpType
 
 P = 128
 PACK = 4
+HALF = 2
 SEQS = 32
 FRAMES = 4
 BONES = 8
@@ -20,183 +22,266 @@ FEATS = 512
 GATES = 3
 BLOCKS = FEATS // P
 COLS = BONES * SEQS
-HALF = 2
+
+FORGET, INPUT, OUTPUT = 0, 1, 2
+GATE_ORDER = (INPUT, FORGET, OUTPUT)
+
+VECTOR_COLS = 320
+
+AHEAD = 3
 
 FLOPS = 2 * GATES * FRAMES * FEATS * FEATS * (COLS + SEQS)
 
 
 def tile_st_hmr_pc_kernel(tc, h_new, c_new, g_s, c_g_s, Wg_s, Zg_s, bg_s, out_0, out_1):
     nc = tc.nc
+    steps = [(t, gate) for t in range(FRAMES) for gate in GATE_ORDER]
     with ExitStack() as ctx:
+        ctx.enter_context(tc.manual_schedule())
         const = ctx.enter_context(tc.tile_pool(name="const", bufs=1))
         raw_pool = ctx.enter_context(tc.tile_pool(name="raw", bufs=1))
-        grouped_pool = ctx.enter_context(tc.tile_pool(name="grouped", bufs=4))
-        code_pool = ctx.enter_context(tc.tile_pool(name="codes", bufs=6))
+        grouped_pool = ctx.enter_context(tc.tile_pool(name="grouped", bufs=6))
+        code_pool = ctx.enter_context(tc.tile_pool(name="codes", bufs=2 * (AHEAD + 1)))
         sig_pool = ctx.enter_context(tc.tile_pool(name="sig", bufs=3))
-        fin_pool = ctx.enter_context(tc.tile_pool(name="fin", bufs=2))
-        turn_psum = ctx.enter_context(tc.psum_pool(name="turn", bufs=2))
-        acc_psum = ctx.enter_context(tc.psum_pool(name="acc", bufs=4))
-        red_psum = ctx.enter_context(tc.psum_pool(name="red", bufs=2))
+        fin_pool = ctx.enter_context(tc.tile_pool(name="fin", bufs=FRAMES))
+        psum = ctx.enter_context(tc.psum_pool(name="psum", bufs=8))
 
         g_sb = const.tile([P, FEATS], BF16)
-        nc.sync.dma_start(out=g_sb[:], in_=g_s.rearrange("b t k -> (b t) k"))
-        h_sb = const.tile([P, BONES * FEATS], BF16)
-        c_sb = const.tile([P, BONES, FEATS], BF16)
+        nc.scalar.dma_start(out=g_sb[:], in_=g_s.rearrange("b t k -> (b t) k"))
         bias_rows = const.tile([P, P], BF16)
         nc.vector.memset(bias_rows[:], 0.0)
+        nc.scalar.dma_start(
+            out=bias_rows[0 : GATES * FRAMES * BLOCKS, :], in_=bg_s.rearrange("g t o (f c) -> (g t o f) c", c=P)
+        )
         cgs_sb = const.tile([P, FRAMES, P], BF16)
+        for f in range(BLOCKS):
+            nc.scalar.dma_start(out=cgs_sb[f * SEQS : (f + 1) * SEQS, :, :], in_=c_g_s[:, :, f * P : (f + 1) * P])
 
-        raw = {}
-        for t in range(FRAMES):
-            for g in range(GATES):
-                for kind, weights in enumerate((Wg_s, Zg_s)):
-                    raw[(t, g, kind)] = raw_pool.tile([P, PACK, FEATS], BF16, name="raw_%d_%d_%d" % (t, g, kind))
-                    nc.sync.dma_start(
-                        out=raw[(t, g, kind)][:], in_=weights[g, t].rearrange("(p j) w -> p j w", j=PACK)
-                    )
-                if t == 0 and g == 0:
-                    nc.sync.dma_start(out=h_sb[:], in_=h_new.rearrange("b t n k -> (b t) (n k)"))
-                    nc.sync.dma_start(
-                        out=bias_rows[0 : GATES * FRAMES * BLOCKS, :],
-                        in_=bg_s.rearrange("g t o (f c) -> (g t o f) c", c=P),
-                    )
-                    nc.sync.dma_start(out=c_sb[:], in_=c_new.rearrange("b t n k -> (b t) n k"))
-                    for f in range(BLOCKS):
-                        nc.sync.dma_start(
-                            out=cgs_sb[f * SEQS : (f + 1) * SEQS, :, :], in_=c_g_s[:, :, f * P : (f + 1) * P]
-                        )
+        h_sb = const.tile([P, BONES * FEATS], BF16)
+        c_sb = const.tile([P, BONES, FEATS], BF16)
+        raw = []
+        for s, (t, gate) in enumerate(steps):
+            pair = []
+            for kind, weights in enumerate((Wg_s, Zg_s)):
+                matrix = raw_pool.tile([P, PACK, FEATS], BF16, name="raw_%d_%d" % (s, kind))
+                nc.sync.dma_start(out=matrix[:], in_=weights[gate, t].rearrange("(p j) w -> p j w", j=PACK))
+                pair.append(matrix)
+            raw.append(pair)
+            if s == AHEAD - 2:
+                nc.sync.dma_start(out=h_sb[:], in_=h_new.rearrange("b t n k -> (b t) (n k)"))
+            if s == AHEAD - 1:
+                nc.sync.dma_start(out=c_sb[:], in_=c_new.rearrange("b t n k -> (b t) n k"))
 
         ident_f32 = const.tile([P, P], F32)
         make_identity(nc, ident_f32[:])
         ident_bf16 = const.tile([P, P], BF16)
         make_identity(nc, ident_bf16[:])
 
-        def quantise_matrix(key, on_scalar):
-            grouped = grouped_pool.tile([P, FEATS, PACK], BF16, align_bytes=64, name="grouped")
-            dst = grouped[:].rearrange("p (c i) j -> p c j i", i=4)
-            src = raw[key][:].rearrange("p j (c i) -> p c j i", i=4)
-            if on_scalar:
-                nc.scalar.copy(out=dst, in_=src)
-            else:
-                nc.vector.tensor_copy(out=dst, in_=src)
-            codes = code_pool.tile([P, FEATS], U32, align_bytes=64, name="codes")
-            scales = code_pool.tile([P, FEATS], U8, align_bytes=64, name="scales")
-            nc.vector.quantize_mx(
-                out=codes[:].bitcast(FP8X4), scales=scales[:], in_=grouped[:].rearrange("p w j -> p (w j)")
-            )
-            return codes, scales
+        grouped = {}
+        operands = {}
+        acc = {}
+        sig = {}
+        red = {}
+        kept = {}
+        cell = {}
+        squashed = {}
+
+        def regroup(s):
+            grouped[s] = []
+            for kind in range(2):
+                tile = grouped_pool.tile([P, FEATS, PACK], BF16, align_bytes=64, name="grouped")
+                dst = tile[:].rearrange("p (c i) j -> p c j i", i=4)
+                src = raw[s][kind][:].rearrange("p j (c i) -> p c j i", i=4)
+                cut = VECTOR_COLS // 4
+                nc.vector.tensor_copy(out=dst[:, :cut], in_=src[:, :cut])
+                nc.scalar.copy(out=dst[:, cut:], in_=src[:, cut:])
+                grouped[s].append(tile)
+
+        def quantise(s):
+            operands[s] = []
+            for kind in range(2):
+                codes = code_pool.tile([P, FEATS], U32, align_bytes=64, name="codes")
+                scales = code_pool.tile([P, FEATS], U8, align_bytes=64, name="scales")
+                nc.vector.quantize_mx(
+                    out=codes[:].bitcast(FP8X4),
+                    scales=scales[:],
+                    in_=grouped[s][kind][:].rearrange("p w j -> p (w j)"),
+                )
+                operands[s].append((codes, scales))
+
+        def gate_matmuls(s):
+            t = steps[s][0]
+            frame_cols = slice(t * COLS, (t + 1) * COLS)
+            moving = ((h_codes, h_scales), (g_codes, g_scales))
+            acc[s] = []
+            for pair in range(BLOCKS // 2):
+                bank = psum.tile([P, 2, COLS], F32, tag="bank", name="acc")
+                for i in range(2):
+                    block_cols = slice((2 * pair + i) * P, (2 * pair + i + 1) * P)
+                    for kind in range(2):
+                        nc.tensor.matmul_mx(
+                            out=bank[:, i, :],
+                            lhsT=operands[s][kind][0][:, block_cols].bitcast(FP8X4),
+                            lhsT_scale=operands[s][kind][1][:, block_cols],
+                            rhs=moving[kind][0][:, frame_cols].bitcast(FP8X4),
+                            rhs_scale=moving[kind][1][:, frame_cols],
+                            start=(kind == 0),
+                            stop=(kind == 1),
+                        )
+                acc[s].append(bank)
+
+        def sigmoids(s):
+            t, gate = steps[s]
+            sig[s] = sig_pool.tile([P, BONES, BLOCKS, SEQS], F32, name="sig")
+            for f in range(BLOCKS):
+                bias_col = (gate * FRAMES + t) * BLOCKS + f
+                nc.scalar.activation(
+                    out=sig[s][:, :, f, :],
+                    in_=acc[s][f // 2][:, f % 2, :].rearrange("p (n b) -> p n b", b=SEQS),
+                    func=ACT.Sigmoid,
+                    bias=bias_sb[:, bias_col : bias_col + 1],
+                )
+
+        def weigh_by_cell(s):
+            t, gate = steps[s]
+            if gate == FORGET:
+                flat = sig[s][:].rearrange("p n f b -> p (n f b)")
+                nc.vector.tensor_mul(out=flat, in0=flat, in1=c_turned_sb[:, t].rearrange("p n f b -> p (n f b)"))
+
+        def sum_over_bones(s):
+            red[s] = psum.tile([P, P], F32, tag="bank", name="red")
+            for n in range(BONES):
+                nc.tensor.matmul(
+                    out=red[s][:],
+                    lhsT=sig[s][:, n].rearrange("p f b -> p (f b)"),
+                    rhs=ident_f32[:],
+                    is_transpose=True,
+                    start=(n == 0),
+                    stop=(n == BONES - 1),
+                )
+
+        def store(out, t, result):
+            for f in range(BLOCKS):
+                nc.sync.dma_start(out=out[:, t, f * P : (f + 1) * P], in_=result[f * SEQS : (f + 1) * SEQS, :])
+
+        def combine(s):
+            t, gate = steps[s]
+            mean = 1.0 / BONES
+            if gate == INPUT:
+                kept[t] = fin_pool.tile([P, P], F32, name="kept")
+                nc.vector.scalar_tensor_tensor(
+                    out=kept[t][:], in0=red[s][:], scalar=mean, in1=cgs_sb[:, t, :], op0=ALU.mult, op1=ALU.mult
+                )
+            if gate == FORGET:
+                cell[t] = fin_pool.tile([P, P], F32, name="cell")
+                nc.vector.scalar_tensor_tensor(
+                    out=cell[t][:], in0=red[s][:], scalar=mean, in1=kept[t][:], op0=ALU.mult, op1=ALU.add
+                )
+                store(out_1, t, cell[t])
+            if gate == OUTPUT:
+                hidden = fin_pool.tile([P, P], F32, name="hidden")
+                nc.vector.scalar_tensor_tensor(
+                    out=hidden[:], in0=red[s][:], scalar=mean, in1=squashed[t][:], op0=ALU.mult, op1=ALU.mult
+                )
+                store(out_0, t, hidden)
+
+        def squash(s):
+            t, gate = steps[s]
+            if gate == FORGET:
+                squashed[t] = fin_pool.tile([P, P], F32, name="squashed")
+                nc.scalar.activation(out=squashed[t][:], in_=cell[t][:], func=ACT.Tanh)
 
         g_words = g_sb[:].bitcast(F32).rearrange("p (q u) -> p u q", u=HALF)
-        g_turned = turn_psum.tile([P, HALF, P], F32, tag="turn")
+        g_turned = psum.tile([P, HALF, P], F32, tag="bank")
         for u in range(HALF):
             nc.tensor.transpose(g_turned[:, u, :], g_words[:, u, :], ident_f32[:])
-        g_grouped = const.tile([P, FRAMES * COLS * PACK], BF16, align_bytes=64)
-        g_grouped_words = g_grouped[:].bitcast(F32).rearrange(
-            "p (t n b u) -> p t n b u", t=FRAMES, n=BONES, u=HALF
+        g_grouped = const.tile([P, FRAMES * SEQS * PACK], BF16, align_bytes=64)
+        nc.scalar.copy(
+            out=g_grouped[:].bitcast(F32).rearrange("p (t b u) -> p t b u", t=FRAMES, u=HALF),
+            in_=g_turned[:].rearrange("p u (b t) -> p t b u", t=FRAMES),
         )
-        for t in range(FRAMES):
-            one_frame = g_turned[:].rearrange("p u (b t) -> p t b u", t=FRAMES)[:, t]
-            nc.scalar.copy(
-                out=g_grouped_words[:, t], in_=one_frame.unsqueeze(1).to_broadcast([P, BONES, SEQS, HALF])
-            )
+        g_codes_once = const.tile([P, FRAMES, 1, SEQS], U32, align_bytes=64)
+        g_scales_once = const.tile([P, FRAMES, 1, SEQS], U8, align_bytes=64)
+        nc.vector.memset(g_scales_once[:].bitcast(I32), 0)
+        nc.vector.quantize_mx(
+            out=g_codes_once[:].rearrange("p t o b -> p (t o b)").bitcast(FP8X4),
+            scales=g_scales_once[:].rearrange("p t o b -> p (t o b)"),
+            in_=g_grouped[:],
+        )
         g_codes = const.tile([P, FRAMES * COLS], U32, align_bytes=64)
         g_scales = const.tile([P, FRAMES * COLS], U8, align_bytes=64)
-        nc.vector.quantize_mx(out=g_codes[:].bitcast(FP8X4), scales=g_scales[:], in_=g_grouped[:])
-
-        h_words = h_sb[:].bitcast(F32).rearrange("p (n q u) -> p n u q", n=BONES, u=HALF)
-        h_grouped = const.tile([P, FRAMES * COLS * PACK], BF16, align_bytes=64)
-        h_grouped_words = h_grouped[:].bitcast(F32).rearrange(
-            "p (t n b u) -> p t n b u", t=FRAMES, n=BONES, u=HALF
+        nc.vector.tensor_copy(
+            out=g_codes[:].bitcast(I32).rearrange("p (t n b) -> p t n b", t=FRAMES, n=BONES),
+            in_=g_codes_once[:].bitcast(I32).to_broadcast([P, FRAMES, BONES, SEQS]),
         )
-        for n in range(BONES):
-            h_turned = turn_psum.tile([P, HALF, P], F32, tag="turn")
-            for u in range(HALF):
-                nc.tensor.transpose(h_turned[:, u, :], h_words[:, n, u, :], ident_f32[:])
-            nc.scalar.copy(
-                out=h_grouped_words[:, :, n], in_=h_turned[:].rearrange("p u (b t) -> p t b u", t=FRAMES)
-            )
-        h_codes = const.tile([P, FRAMES * COLS], U32, align_bytes=64)
-        h_scales = const.tile([P, FRAMES * COLS], U8, align_bytes=64)
-        nc.vector.quantize_mx(out=h_codes[:].bitcast(FP8X4), scales=h_scales[:], in_=h_grouped[:])
+        nc.vector.tensor_copy(
+            out=g_scales[:].bitcast(I32).rearrange("p (t n b) -> p t n b", t=FRAMES, n=BONES),
+            in_=g_scales_once[:].bitcast(I32).to_broadcast([P, FRAMES, BONES, SEQS // 4]),
+        )
 
-        bias_turned = turn_psum.tile([P, P], BF16, tag="turn")
+        bias_turned = psum.tile([P, P], BF16, tag="bank")
         nc.tensor.transpose(bias_turned[:], bias_rows[:], ident_bf16[:])
         bias_sb = const.tile([P, GATES * FRAMES * BLOCKS], F32)
         nc.vector.tensor_copy(out=bias_sb[:], in_=bias_turned[:, 0 : GATES * FRAMES * BLOCKS])
 
-        c_turned_sb = const.tile([P, FRAMES, BONES, BLOCKS, SEQS], BF16)
+        h_words = h_sb[:].bitcast(F32).rearrange("p (n q u) -> p n u q", n=BONES, u=HALF)
+        h_turned = []
         for n in range(BONES):
-            c_turned = turn_psum.tile([P, BLOCKS, P], BF16, tag="turn")
+            if n % 2 == 0:
+                h_turned.append(psum.tile([P, 2, HALF, P], F32, tag="bank", name="h_turned"))
+            for u in range(HALF):
+                nc.tensor.transpose(h_turned[n // 2][:, n % 2, u, :], h_words[:, n, u, :], ident_f32[:])
+        c_turned = []
+        for n in range(BONES):
+            if n % 2 == 0:
+                c_turned.append(psum.tile([P, 2, BLOCKS, P], BF16, tag="bank", name="c_turned"))
             for f in range(BLOCKS):
-                nc.tensor.transpose(c_turned[:, f, :], c_sb[:, n, f * P : (f + 1) * P], ident_bf16[:])
-            nc.scalar.copy(
-                out=c_turned_sb[:, :, n], in_=c_turned[:].rearrange("p f (b t) -> p t f b", t=FRAMES)
-            )
+                nc.tensor.transpose(c_turned[n // 2][:, n % 2, f, :], c_sb[:, n, f * P : (f + 1) * P], ident_bf16[:])
 
-        count = 0
+        for s in range(AHEAD):
+            regroup(s)
+            quantise(s)
+
+        def out_of_psum(n, out, in_):
+            if (n // 2) % 2 == 0:
+                nc.scalar.copy(out=out, in_=in_)
+            else:
+                nc.vector.tensor_copy(out=out, in_=in_)
+
+        h_grouped = const.tile([P, FRAMES, COLS * PACK], BF16, align_bytes=64)
+        h_grouped_words = h_grouped[:].bitcast(F32).rearrange("p t (n b u) -> p t n b u", n=BONES, u=HALF)
+        for n in range(BONES):
+            out_of_psum(
+                n, h_grouped_words[:, :, n], h_turned[n // 2][:, n % 2].rearrange("p u (b t) -> p t b u", t=FRAMES)
+            )
+        h_codes = const.tile([P, FRAMES * COLS], U32, align_bytes=64)
+        h_scales = const.tile([P, FRAMES * COLS], U8, align_bytes=64)
         for t in range(FRAMES):
             frame_cols = slice(t * COLS, (t + 1) * COLS)
-            red = red_psum.tile([P, GATES, P], F32)
-            for g in range(GATES):
-                operands = []
-                for kind in range(2):
-                    operands.append(quantise_matrix((t, g, kind), on_scalar=(count % 3 == 1)))
-                    count += 1
-                moving = ((h_codes, h_scales), (g_codes, g_scales))
-                sig = sig_pool.tile([P, BONES, BLOCKS, SEQS], F32)
-                for pair in range(BLOCKS // 2):
-                    acc = acc_psum.tile([P, 2, COLS], F32)
-                    for i in range(2):
-                        block_cols = slice((2 * pair + i) * P, (2 * pair + i + 1) * P)
-                        for kind in range(2):
-                            nc.tensor.matmul_mx(
-                                out=acc[:, i, :],
-                                lhsT=operands[kind][0][:, block_cols].bitcast(FP8X4),
-                                lhsT_scale=operands[kind][1][:, block_cols],
-                                rhs=moving[kind][0][:, frame_cols].bitcast(FP8X4),
-                                rhs_scale=moving[kind][1][:, frame_cols],
-                                start=(kind == 0),
-                                stop=(kind == 1),
-                            )
-                    for i in range(2):
-                        f = 2 * pair + i
-                        bias_col = (g * FRAMES + t) * BLOCKS + f
-                        nc.scalar.activation(
-                            out=sig[:, :, f, :],
-                            in_=acc[:, i, :].rearrange("p (n b) -> p n b", b=SEQS),
-                            func=ACT.Sigmoid,
-                            bias=bias_sb[:, bias_col : bias_col + 1],
-                        )
-                if g == 0:
-                    flat = sig[:].rearrange("p n f b -> p (n f b)")
-                    nc.vector.tensor_mul(
-                        out=flat, in0=flat, in1=c_turned_sb[:, t].rearrange("p n f b -> p (n f b)")
-                    )
-                for n in range(BONES):
-                    nc.tensor.matmul(
-                        out=red[:, g, :],
-                        lhsT=sig[:, n].rearrange("p f b -> p (f b)"),
-                        rhs=ident_f32[:],
-                        is_transpose=True,
-                        start=(n == 0),
-                        stop=(n == BONES - 1),
-                    )
+            nc.vector.quantize_mx(
+                out=h_codes[:, frame_cols].bitcast(FP8X4), scales=h_scales[:, frame_cols], in_=h_grouped[:, t, :]
+            )
 
-            kept = fin_pool.tile([P, P], F32)
-            nc.vector.scalar_tensor_tensor(
-                out=kept[:], in0=red[:, 1, :], scalar=1.0 / BONES, in1=cgs_sb[:, t, :], op0=ALU.mult, op1=ALU.mult
+        c_turned_sb = const.tile([P, FRAMES, BONES, BLOCKS, SEQS], BF16)
+        for n in range(BONES):
+            out_of_psum(
+                n, c_turned_sb[:, :, n], c_turned[n // 2][:, n % 2].rearrange("p f (b t) -> p t f b", t=FRAMES)
             )
-            cell = fin_pool.tile([P, P], F32)
-            nc.vector.scalar_tensor_tensor(
-                out=cell[:], in0=red[:, 0, :], scalar=1.0 / BONES, in1=kept[:], op0=ALU.mult, op1=ALU.add
-            )
-            squashed = fin_pool.tile([P, P], F32)
-            nc.scalar.activation(out=squashed[:], in_=cell[:], func=ACT.Tanh)
-            hidden = fin_pool.tile([P, P], F32)
-            nc.vector.scalar_tensor_tensor(
-                out=hidden[:], in0=red[:, 2, :], scalar=1.0 / BONES, in1=squashed[:], op0=ALU.mult, op1=ALU.mult
-            )
-            for f in range(BLOCKS):
-                rows = slice(f * SEQS, (f + 1) * SEQS)
-                nc.sync.dma_start(out=out_1[:, t, f * P : (f + 1) * P], in_=cell[rows, :])
-                nc.sync.dma_start(out=out_0[:, t, f * P : (f + 1) * P], in_=hidden[rows, :])
+
+        for s in range(len(steps) + 1):
+            if s + AHEAD < len(steps):
+                regroup(s + AHEAD)
+            if s >= 1:
+                weigh_by_cell(s - 1)
+            if s + AHEAD < len(steps):
+                quantise(s + AHEAD)
+            if s < len(steps):
+                gate_matmuls(s)
+            if s >= 1:
+                sum_over_bones(s - 1)
+            if s >= 2:
+                squash(s - 2)
+            if s < len(steps):
+                sigmoids(s)
+            if s >= 1:
+                combine(s - 1)

@@ -22,13 +22,17 @@ FEATS = 512
 GATES = 3
 BLOCKS = FEATS // P
 COLS = BONES * SEQS
+W, Z = 0, 1
 
 FORGET, INPUT, OUTPUT = 0, 1, 2
 GATE_ORDER = (INPUT, FORGET, OUTPUT)
 
-VECTOR_COLS = 320
+SCALAR_COLS = 416
 
-AHEAD = 3
+AHEAD = 2
+
+LOAD_H_BEHIND = 1
+LOAD_C_BEHIND = 2
 
 FLOPS = 2 * GATES * FRAMES * FEATS * FEATS * (COLS + SEQS)
 
@@ -40,37 +44,38 @@ def tile_st_hmr_pc_kernel(tc, h_new, c_new, g_s, c_g_s, Wg_s, Zg_s, bg_s, out_0,
         ctx.enter_context(tc.manual_schedule())
         const = ctx.enter_context(tc.tile_pool(name="const", bufs=1))
         raw_pool = ctx.enter_context(tc.tile_pool(name="raw", bufs=1))
-        grouped_pool = ctx.enter_context(tc.tile_pool(name="grouped", bufs=6))
-        code_pool = ctx.enter_context(tc.tile_pool(name="codes", bufs=2 * (AHEAD + 1)))
+        grouped_pool = ctx.enter_context(tc.tile_pool(name="grouped", bufs=3))
+        code_pool = ctx.enter_context(tc.tile_pool(name="codes", bufs=AHEAD + 1))
         sig_pool = ctx.enter_context(tc.tile_pool(name="sig", bufs=3))
         fin_pool = ctx.enter_context(tc.tile_pool(name="fin", bufs=FRAMES))
         psum = ctx.enter_context(tc.psum_pool(name="psum", bufs=8))
 
         g_sb = const.tile([P, FEATS], BF16)
-        nc.scalar.dma_start(out=g_sb[:], in_=g_s.rearrange("b t k -> (b t) k"))
-        bias_rows = const.tile([P, P], BF16)
-        nc.vector.memset(bias_rows[:], 0.0)
-        nc.scalar.dma_start(
-            out=bias_rows[0 : GATES * FRAMES * BLOCKS, :], in_=bg_s.rearrange("g t o (f c) -> (g t o f) c", c=P)
-        )
-        cgs_sb = const.tile([P, FRAMES, P], BF16)
-        for f in range(BLOCKS):
-            nc.scalar.dma_start(out=cgs_sb[f * SEQS : (f + 1) * SEQS, :, :], in_=c_g_s[:, :, f * P : (f + 1) * P])
-
         h_sb = const.tile([P, BONES * FEATS], BF16)
         c_sb = const.tile([P, BONES, FEATS], BF16)
+        bias_rows = const.tile([P, P], BF16)
+        cgs_sb = const.tile([P, FRAMES, P], BF16)
+        nc.vector.memset(bias_rows[:], 0.0)
+        nc.sync.dma_start(out=g_sb[:], in_=g_s.rearrange("b t k -> (b t) k"))
         raw = []
         for s, (t, gate) in enumerate(steps):
-            pair = []
-            for kind, weights in enumerate((Wg_s, Zg_s)):
-                matrix = raw_pool.tile([P, PACK, FEATS], BF16, name="raw_%d_%d" % (s, kind))
-                nc.sync.dma_start(out=matrix[:], in_=weights[gate, t].rearrange("(p j) w -> p j w", j=PACK))
-                pair.append(matrix)
-            raw.append(pair)
-            if s == AHEAD - 2:
+            raw.append(raw_pool.tile([P, PACK, 2, FEATS], BF16, name="raw_%d" % s))
+            for kind, weights in ((W, Wg_s), (Z, Zg_s)):
+                nc.sync.dma_start(
+                    out=raw[s][:, :, kind, :], in_=weights[gate, t].rearrange("(p j) w -> p j w", j=PACK)
+                )
+            if s == LOAD_H_BEHIND:
                 nc.sync.dma_start(out=h_sb[:], in_=h_new.rearrange("b t n k -> (b t) (n k)"))
-            if s == AHEAD - 1:
+                nc.sync.dma_start(
+                    out=bias_rows[0 : GATES * FRAMES * BLOCKS, :],
+                    in_=bg_s.rearrange("g t o (f c) -> (g t o f) c", c=P),
+                )
+            if s == LOAD_C_BEHIND:
                 nc.sync.dma_start(out=c_sb[:], in_=c_new.rearrange("b t n k -> (b t) n k"))
+                for f in range(BLOCKS):
+                    nc.sync.dma_start(
+                        out=cgs_sb[f * SEQS : (f + 1) * SEQS, :, :], in_=c_g_s[:, :, f * P : (f + 1) * P]
+                    )
 
         ident_f32 = const.tile([P, P], F32)
         make_identity(nc, ident_f32[:])
@@ -78,57 +83,52 @@ def tile_st_hmr_pc_kernel(tc, h_new, c_new, g_s, c_g_s, Wg_s, Zg_s, bg_s, out_0,
         make_identity(nc, ident_bf16[:])
 
         grouped = {}
-        operands = {}
+        codes = {}
+        scales = {}
         acc = {}
         sig = {}
         red = {}
         kept = {}
         cell = {}
         squashed = {}
+        c_turned = []
 
         def regroup(s):
-            grouped[s] = []
-            for kind in range(2):
-                tile = grouped_pool.tile([P, FEATS, PACK], BF16, align_bytes=64, name="grouped")
-                dst = tile[:].rearrange("p (c i) j -> p c j i", i=4)
-                src = raw[s][kind][:].rearrange("p j (c i) -> p c j i", i=4)
-                cut = VECTOR_COLS // 4
-                nc.vector.tensor_copy(out=dst[:, :cut], in_=src[:, :cut])
-                nc.scalar.copy(out=dst[:, cut:], in_=src[:, cut:])
-                grouped[s].append(tile)
+            grouped[s] = grouped_pool.tile([P, 2, FEATS, PACK], BF16, align_bytes=64, name="grouped")
+            dst = grouped[s][:].rearrange("p m (c i) j -> p (m c) j i", i=4)
+            src = raw[s][:].rearrange("p j m (c i) -> p (m c) j i", i=4)
+            cut = (2 * FEATS - SCALAR_COLS) // 4
+            nc.vector.tensor_copy(out=dst[:, :cut], in_=src[:, :cut])
+            nc.scalar.copy(out=dst[:, cut:], in_=src[:, cut:])
 
         def quantise(s):
-            operands[s] = []
-            for kind in range(2):
-                codes = code_pool.tile([P, FEATS], U32, align_bytes=64, name="codes")
-                scales = code_pool.tile([P, FEATS], U8, align_bytes=64, name="scales")
-                nc.vector.quantize_mx(
-                    out=codes[:].bitcast(FP8X4),
-                    scales=scales[:],
-                    in_=grouped[s][kind][:].rearrange("p w j -> p (w j)"),
-                )
-                operands[s].append((codes, scales))
+            codes[s] = code_pool.tile([P, 2, FEATS], U32, align_bytes=64, name="codes")
+            scales[s] = code_pool.tile([P, 2, FEATS], U8, align_bytes=64, name="scales")
+            nc.vector.quantize_mx(
+                out=codes[s][:].rearrange("p m w -> p (m w)").bitcast(FP8X4),
+                scales=scales[s][:].rearrange("p m w -> p (m w)"),
+                in_=grouped[s][:].rearrange("p m w j -> p (m w j)"),
+            )
 
         def gate_matmuls(s):
             t = steps[s][0]
             frame_cols = slice(t * COLS, (t + 1) * COLS)
-            moving = ((h_codes, h_scales), (g_codes, g_scales))
+            moving = {W: (h_codes, h_scales), Z: (g_codes, g_scales)}
             acc[s] = []
-            for pair in range(BLOCKS // 2):
-                bank = psum.tile([P, 2, COLS], F32, tag="bank", name="acc")
-                for i in range(2):
-                    block_cols = slice((2 * pair + i) * P, (2 * pair + i + 1) * P)
-                    for kind in range(2):
-                        nc.tensor.matmul_mx(
-                            out=bank[:, i, :],
-                            lhsT=operands[s][kind][0][:, block_cols].bitcast(FP8X4),
-                            lhsT_scale=operands[s][kind][1][:, block_cols],
-                            rhs=moving[kind][0][:, frame_cols].bitcast(FP8X4),
-                            rhs_scale=moving[kind][1][:, frame_cols],
-                            start=(kind == 0),
-                            stop=(kind == 1),
-                        )
-                acc[s].append(bank)
+            for f in range(BLOCKS):
+                if f % 2 == 0:
+                    acc[s].append(psum.tile([P, 2, COLS], F32, tag="bank", name="acc"))
+                block_cols = slice(f * P, (f + 1) * P)
+                for kind in (W, Z):
+                    nc.tensor.matmul_mx(
+                        out=acc[s][f // 2][:, f % 2, :],
+                        lhsT=codes[s][:, kind, block_cols].bitcast(FP8X4),
+                        lhsT_scale=scales[s][:, kind, block_cols],
+                        rhs=moving[kind][0][:, frame_cols].bitcast(FP8X4),
+                        rhs_scale=moving[kind][1][:, frame_cols],
+                        start=(kind == W),
+                        stop=(kind == Z),
+                    )
 
         def sigmoids(s):
             t, gate = steps[s]
@@ -145,8 +145,9 @@ def tile_st_hmr_pc_kernel(tc, h_new, c_new, g_s, c_g_s, Wg_s, Zg_s, bg_s, out_0,
         def weigh_by_cell(s):
             t, gate = steps[s]
             if gate == FORGET:
-                flat = sig[s][:].rearrange("p n f b -> p (n f b)")
-                nc.vector.tensor_mul(out=flat, in0=flat, in1=c_turned_sb[:, t].rearrange("p n f b -> p (n f b)"))
+                gate_view = sig[s][:].rearrange("p n f b -> p (n f) b")
+                cell_view = c_turned_sb[:].rearrange("p n f (b t) -> p t (n f) b", t=FRAMES)
+                nc.vector.tensor_mul(out=gate_view, in0=gate_view, in1=cell_view[:, t])
 
         def sum_over_bones(s):
             red[s] = psum.tile([P, P], F32, tag="bank", name="red")
@@ -219,69 +220,69 @@ def tile_st_hmr_pc_kernel(tc, h_new, c_new, g_s, c_g_s, Wg_s, Zg_s, bg_s, out_0,
             in_=g_scales_once[:].bitcast(I32).to_broadcast([P, FRAMES, BONES, SEQS // 4]),
         )
 
-        bias_turned = psum.tile([P, P], BF16, tag="bank")
-        nc.tensor.transpose(bias_turned[:], bias_rows[:], ident_bf16[:])
+        h_grouped = const.tile([P, FRAMES * COLS * PACK], BF16, align_bytes=64)
+        h_codes = const.tile([P, FRAMES * COLS], U32, align_bytes=64)
+        h_scales = const.tile([P, FRAMES * COLS], U8, align_bytes=64)
         bias_sb = const.tile([P, GATES * FRAMES * BLOCKS], F32)
-        nc.vector.tensor_copy(out=bias_sb[:], in_=bias_turned[:, 0 : GATES * FRAMES * BLOCKS])
+        c_turned_sb = const.tile([P, BONES, BLOCKS, P], BF16)
 
-        h_words = h_sb[:].bitcast(F32).rearrange("p (n q u) -> p n u q", n=BONES, u=HALF)
-        h_turned = []
-        for n in range(BONES):
-            if n % 2 == 0:
-                h_turned.append(psum.tile([P, 2, HALF, P], F32, tag="bank", name="h_turned"))
-            for u in range(HALF):
-                nc.tensor.transpose(h_turned[n // 2][:, n % 2, u, :], h_words[:, n, u, :], ident_f32[:])
-        c_turned = []
-        for n in range(BONES):
-            if n % 2 == 0:
-                c_turned.append(psum.tile([P, 2, BLOCKS, P], BF16, tag="bank", name="c_turned"))
-            for f in range(BLOCKS):
-                nc.tensor.transpose(c_turned[n // 2][:, n % 2, f, :], c_sb[:, n, f * P : (f + 1) * P], ident_bf16[:])
+        def turn_h():
+            h_words = h_sb[:].bitcast(F32).rearrange("p (n q u) -> p n u q", n=BONES, u=HALF)
+            words = h_grouped[:].bitcast(F32).rearrange("p (t a x u) -> p a t x u", t=FRAMES, a=BONES // 2, u=HALF)
+            h_turned = []
+            for n in range(BONES):
+                if n % 2 == 0:
+                    h_turned.append(psum.tile([P, HALF, 2, P], F32, tag="bank", name="h_turned"))
+                for u in range(HALF):
+                    nc.tensor.transpose(h_turned[n // 2][:, u, n % 2, :], h_words[:, n, u, :], ident_f32[:])
+            for a in range(BONES // 2):
+                nc.scalar.copy(out=words[:, a], in_=h_turned[a][:].rearrange("p u n (b t) -> p t (n b) u", t=FRAMES))
+
+        def turn_bias():
+            bias_turned = psum.tile([P, P], BF16, tag="bank")
+            nc.tensor.transpose(bias_turned[:], bias_rows[:], ident_bf16[:])
+            nc.scalar.copy(out=bias_sb[:], in_=bias_turned[:, 0 : GATES * FRAMES * BLOCKS])
+
+        def turn_c_on_tensor():
+            for n in range(BONES):
+                if n % 2 == 0:
+                    c_turned.append(psum.tile([P, 2, BLOCKS, P], BF16, tag="bank", name="c_turned"))
+                for f in range(BLOCKS):
+                    nc.tensor.transpose(
+                        c_turned[n // 2][:, n % 2, f, :], c_sb[:, n, f * P : (f + 1) * P], ident_bf16[:]
+                    )
+
+        def c_out_of_psum():
+            for a in range(BONES // 2):
+                nc.scalar.copy(out=c_turned_sb[:, 2 * a : 2 * a + 2], in_=c_turned[a][:])
 
         for s in range(AHEAD):
             regroup(s)
+        for s in range(AHEAD - 1):
             quantise(s)
-
-        def out_of_psum(n, out, in_):
-            if (n // 2) % 2 == 0:
-                nc.scalar.copy(out=out, in_=in_)
-            else:
-                nc.vector.tensor_copy(out=out, in_=in_)
-
-        h_grouped = const.tile([P, FRAMES, COLS * PACK], BF16, align_bytes=64)
-        h_grouped_words = h_grouped[:].bitcast(F32).rearrange("p t (n b u) -> p t n b u", n=BONES, u=HALF)
-        for n in range(BONES):
-            out_of_psum(
-                n, h_grouped_words[:, :, n], h_turned[n // 2][:, n % 2].rearrange("p u (b t) -> p t b u", t=FRAMES)
-            )
-        h_codes = const.tile([P, FRAMES * COLS], U32, align_bytes=64)
-        h_scales = const.tile([P, FRAMES * COLS], U8, align_bytes=64)
-        for t in range(FRAMES):
-            frame_cols = slice(t * COLS, (t + 1) * COLS)
-            nc.vector.quantize_mx(
-                out=h_codes[:, frame_cols].bitcast(FP8X4), scales=h_scales[:, frame_cols], in_=h_grouped[:, t, :]
-            )
-
-        c_turned_sb = const.tile([P, FRAMES, BONES, BLOCKS, SEQS], BF16)
-        for n in range(BONES):
-            out_of_psum(
-                n, c_turned_sb[:, :, n], c_turned[n // 2][:, n % 2].rearrange("p f (b t) -> p t f b", t=FRAMES)
-            )
+        turn_h()
+        turn_bias()
 
         for s in range(len(steps) + 1):
             if s + AHEAD < len(steps):
                 regroup(s + AHEAD)
+            if s == 0:
+                nc.vector.quantize_mx(out=h_codes[:].bitcast(FP8X4), scales=h_scales[:], in_=h_grouped[:])
             if s >= 1:
                 weigh_by_cell(s - 1)
-            if s + AHEAD < len(steps):
-                quantise(s + AHEAD)
+            if s + AHEAD - 1 < len(steps):
+                quantise(s + AHEAD - 1)
             if s < len(steps):
                 gate_matmuls(s)
+            if s == 0:
+                turn_c_on_tensor()
             if s >= 1:
                 sum_over_bones(s - 1)
             if s >= 2:
                 squash(s - 2)
             if s < len(steps):
                 sigmoids(s)
+            if s == 0:
+                c_out_of_psum()
             if s >= 1:
                 combine(s - 1)

@@ -27,11 +27,11 @@ W, Z = 0, 1
 FORGET, INPUT, OUTPUT = 0, 1, 2
 GATE_ORDER = (INPUT, FORGET, OUTPUT)
 
-SCALAR_COLS = 416
+SCALAR_COLS = 192
 
 AHEAD = 2
 
-LOAD_H_BEHIND = 1
+LOAD_H_BEHIND = 0
 LOAD_C_BEHIND = 2
 
 FLOPS = 2 * GATES * FRAMES * FEATS * FEATS * (COLS + SEQS)
@@ -59,11 +59,9 @@ def tile_st_hmr_pc_kernel(tc, h_new, c_new, g_s, c_g_s, Wg_s, Zg_s, bg_s, out_0,
         nc.sync.dma_start(out=g_sb[:], in_=g_s.rearrange("b t k -> (b t) k"))
         raw = []
         for s, (t, gate) in enumerate(steps):
-            raw.append(raw_pool.tile([P, PACK, 2, FEATS], BF16, name="raw_%d" % s))
+            raw.append(raw_pool.tile([P, 2, PACK, FEATS], BF16, name="raw_%d" % s))
             for kind, weights in ((W, Wg_s), (Z, Zg_s)):
-                nc.sync.dma_start(
-                    out=raw[s][:, :, kind, :], in_=weights[gate, t].rearrange("(p j) w -> p j w", j=PACK)
-                )
+                nc.sync.dma_start(out=raw[s][:, kind], in_=weights[gate, t].rearrange("(p j) w -> p j w", j=PACK))
             if s == LOAD_H_BEHIND:
                 nc.sync.dma_start(out=h_sb[:], in_=h_new.rearrange("b t n k -> (b t) (n k)"))
                 nc.sync.dma_start(
@@ -95,11 +93,12 @@ def tile_st_hmr_pc_kernel(tc, h_new, c_new, g_s, c_g_s, Wg_s, Zg_s, bg_s, out_0,
 
         def regroup(s):
             grouped[s] = grouped_pool.tile([P, 2, FEATS, PACK], BF16, align_bytes=64, name="grouped")
-            dst = grouped[s][:].rearrange("p m (c i) j -> p (m c) j i", i=4)
-            src = raw[s][:].rearrange("p j m (c i) -> p (m c) j i", i=4)
-            cut = (2 * FEATS - SCALAR_COLS) // 4
-            nc.vector.tensor_copy(out=dst[:, :cut], in_=src[:, :cut])
-            nc.scalar.copy(out=dst[:, cut:], in_=src[:, cut:])
+            dst = grouped[s][:].rearrange("p m (c i) j -> p m c j i", i=4)
+            src = raw[s][:].rearrange("p m j (c i) -> p m c j i", i=4)
+            cut = (FEATS - SCALAR_COLS) // 4
+            nc.vector.tensor_copy(out=dst[:, :, :cut], in_=src[:, :, :cut])
+            for kind in (W, Z):
+                nc.scalar.copy(out=dst[:, kind, cut:], in_=src[:, kind, cut:])
 
         def quantise(s):
             codes[s] = code_pool.tile([P, 2, FEATS], U32, align_bytes=64, name="codes")
@@ -258,16 +257,16 @@ def tile_st_hmr_pc_kernel(tc, h_new, c_new, g_s, c_g_s, Wg_s, Zg_s, bg_s, out_0,
 
         for s in range(AHEAD):
             regroup(s)
+            if s == LOAD_H_BEHIND:
+                turn_h()
+                turn_bias()
+        nc.vector.quantize_mx(out=h_codes[:].bitcast(FP8X4), scales=h_scales[:], in_=h_grouped[:])
         for s in range(AHEAD - 1):
             quantise(s)
-        turn_h()
-        turn_bias()
 
         for s in range(len(steps) + 1):
             if s + AHEAD < len(steps):
                 regroup(s + AHEAD)
-            if s == 0:
-                nc.vector.quantize_mx(out=h_codes[:].bitcast(FP8X4), scales=h_scales[:], in_=h_grouped[:])
             if s >= 1:
                 weigh_by_cell(s - 1)
             if s + AHEAD - 1 < len(steps):

@@ -27,7 +27,7 @@ W, Z = 0, 1
 FORGET, INPUT, OUTPUT = 0, 1, 2
 GATE_ORDER = (INPUT, FORGET, OUTPUT)
 
-SCALAR_COLS = 192
+SCALAR_COLS = 224
 
 AHEAD = 2
 

@@ -14,7 +14,11 @@ ALU = mybir.AluOpType
 
 P = 128
 PACK = 4
-HALF = 2
+PAIRS = 2
+RUN = 4
+SCALES_PER_I32 = 4
+GROUPS_PER_BANK = 2
+BONES_PER_BANK = 2
 SEQS = 32
 FRAMES = 4
 BONES = 8
@@ -23,16 +27,18 @@ GATES = 3
 BLOCKS = FEATS // P
 COLS = BONES * SEQS
 W, Z = 0, 1
+KINDS = 2
 
 FORGET, INPUT, OUTPUT = 0, 1, 2
 GATE_ORDER = (INPUT, FORGET, OUTPUT)
 
-SCALAR_COLS = 224
+SCALAR_COLS = 256
 
-AHEAD = 2
+AHEAD = 3
+SUMS_BEHIND = 2
 
-LOAD_H_BEHIND = 0
-LOAD_C_BEHIND = 2
+LOAD_H_BEHIND = 1
+LOAD_C_BEHIND = 3
 
 FLOPS = 2 * GATES * FRAMES * FEATS * FEATS * (COLS + SEQS)
 
@@ -46,7 +52,7 @@ def tile_st_hmr_pc_kernel(tc, h_new, c_new, g_s, c_g_s, Wg_s, Zg_s, bg_s, out_0,
         raw_pool = ctx.enter_context(tc.tile_pool(name="raw", bufs=1))
         grouped_pool = ctx.enter_context(tc.tile_pool(name="grouped", bufs=3))
         code_pool = ctx.enter_context(tc.tile_pool(name="codes", bufs=AHEAD + 1))
-        sig_pool = ctx.enter_context(tc.tile_pool(name="sig", bufs=3))
+        sig_pool = ctx.enter_context(tc.tile_pool(name="sig", bufs=SUMS_BEHIND + 2))
         fin_pool = ctx.enter_context(tc.tile_pool(name="fin", bufs=FRAMES))
         psum = ctx.enter_context(tc.psum_pool(name="psum", bufs=8))
 
@@ -59,7 +65,7 @@ def tile_st_hmr_pc_kernel(tc, h_new, c_new, g_s, c_g_s, Wg_s, Zg_s, bg_s, out_0,
         nc.sync.dma_start(out=g_sb[:], in_=g_s.rearrange("b t k -> (b t) k"))
         raw = []
         for s, (t, gate) in enumerate(steps):
-            raw.append(raw_pool.tile([P, 2, PACK, FEATS], BF16, name="raw_%d" % s))
+            raw.append(raw_pool.tile([P, KINDS, PACK, FEATS], BF16, name="raw_%d" % s))
             for kind, weights in ((W, Wg_s), (Z, Zg_s)):
                 nc.sync.dma_start(out=raw[s][:, kind], in_=weights[gate, t].rearrange("(p j) w -> p j w", j=PACK))
             if s == LOAD_H_BEHIND:
@@ -89,20 +95,19 @@ def tile_st_hmr_pc_kernel(tc, h_new, c_new, g_s, c_g_s, Wg_s, Zg_s, bg_s, out_0,
         kept = {}
         cell = {}
         squashed = {}
-        c_turned = []
 
         def regroup(s):
-            grouped[s] = grouped_pool.tile([P, 2, FEATS, PACK], BF16, align_bytes=64, name="grouped")
-            dst = grouped[s][:].rearrange("p m (c i) j -> p m c j i", i=4)
-            src = raw[s][:].rearrange("p m j (c i) -> p m c j i", i=4)
-            cut = (FEATS - SCALAR_COLS) // 4
+            grouped[s] = grouped_pool.tile([P, KINDS, FEATS, PACK], BF16, align_bytes=64, name="grouped")
+            dst = grouped[s][:].rearrange("p m (v i) j -> p m v j i", i=RUN)
+            src = raw[s][:].rearrange("p m j (v i) -> p m v j i", i=RUN)
+            cut = (FEATS - SCALAR_COLS) // RUN
             nc.vector.tensor_copy(out=dst[:, :, :cut], in_=src[:, :, :cut])
             for kind in (W, Z):
                 nc.scalar.copy(out=dst[:, kind, cut:], in_=src[:, kind, cut:])
 
         def quantise(s):
-            codes[s] = code_pool.tile([P, 2, FEATS], U32, align_bytes=64, name="codes")
-            scales[s] = code_pool.tile([P, 2, FEATS], U8, align_bytes=64, name="scales")
+            codes[s] = code_pool.tile([P, KINDS, FEATS], U32, align_bytes=64, name="codes")
+            scales[s] = code_pool.tile([P, KINDS, FEATS], U8, align_bytes=64, name="scales")
             nc.vector.quantize_mx(
                 out=codes[s][:].rearrange("p m w -> p (m w)").bitcast(FP8X4),
                 scales=scales[s][:].rearrange("p m w -> p (m w)"),
@@ -115,12 +120,12 @@ def tile_st_hmr_pc_kernel(tc, h_new, c_new, g_s, c_g_s, Wg_s, Zg_s, bg_s, out_0,
             moving = {W: (h_codes, h_scales), Z: (g_codes, g_scales)}
             acc[s] = []
             for f in range(BLOCKS):
-                if f % 2 == 0:
-                    acc[s].append(psum.tile([P, 2, COLS], F32, tag="bank", name="acc"))
+                if f % GROUPS_PER_BANK == 0:
+                    acc[s].append(psum.tile([P, GROUPS_PER_BANK, COLS], F32, tag="bank", name="acc"))
                 block_cols = slice(f * P, (f + 1) * P)
                 for kind in (W, Z):
                     nc.tensor.matmul_mx(
-                        out=acc[s][f // 2][:, f % 2, :],
+                        out=acc[s][f // GROUPS_PER_BANK][:, f % GROUPS_PER_BANK, :],
                         lhsT=codes[s][:, kind, block_cols].bitcast(FP8X4),
                         lhsT_scale=scales[s][:, kind, block_cols],
                         rhs=moving[kind][0][:, frame_cols].bitcast(FP8X4),
@@ -136,17 +141,17 @@ def tile_st_hmr_pc_kernel(tc, h_new, c_new, g_s, c_g_s, Wg_s, Zg_s, bg_s, out_0,
                 bias_col = (gate * FRAMES + t) * BLOCKS + f
                 nc.scalar.activation(
                     out=sig[s][:, :, f, :],
-                    in_=acc[s][f // 2][:, f % 2, :].rearrange("p (n b) -> p n b", b=SEQS),
+                    in_=acc[s][f // GROUPS_PER_BANK][:, f % GROUPS_PER_BANK, :].rearrange("p (n b) -> p n b", b=SEQS),
                     func=ACT.Sigmoid,
                     bias=bias_sb[:, bias_col : bias_col + 1],
                 )
 
-        def weigh_by_cell(s):
+        def weigh_by_c_new(s):
             t, gate = steps[s]
             if gate == FORGET:
                 gate_view = sig[s][:].rearrange("p n f b -> p (n f) b")
-                cell_view = c_turned_sb[:].rearrange("p n f (b t) -> p t (n f) b", t=FRAMES)
-                nc.vector.tensor_mul(out=gate_view, in0=gate_view, in1=cell_view[:, t])
+                c_view = c_turned_sb[:].rearrange("p n f (b t) -> p t (n f) b", t=FRAMES)
+                nc.vector.tensor_mul(out=gate_view, in0=gate_view, in1=c_view[:, t])
 
         def sum_over_bones(s):
             red[s] = psum.tile([P, P], F32, tag="bank", name="red")
@@ -191,13 +196,13 @@ def tile_st_hmr_pc_kernel(tc, h_new, c_new, g_s, c_g_s, Wg_s, Zg_s, bg_s, out_0,
                 squashed[t] = fin_pool.tile([P, P], F32, name="squashed")
                 nc.scalar.activation(out=squashed[t][:], in_=cell[t][:], func=ACT.Tanh)
 
-        g_words = g_sb[:].bitcast(F32).rearrange("p (q u) -> p u q", u=HALF)
-        g_turned = psum.tile([P, HALF, P], F32, tag="bank")
-        for u in range(HALF):
-            nc.tensor.transpose(g_turned[:, u, :], g_words[:, u, :], ident_f32[:])
+        g_pairs = g_sb[:].bitcast(F32).rearrange("p (q u) -> p u q", u=PAIRS)
+        g_turned = psum.tile([P, PAIRS, P], F32, tag="bank")
+        for u in range(PAIRS):
+            nc.tensor.transpose(g_turned[:, u, :], g_pairs[:, u, :], ident_f32[:])
         g_grouped = const.tile([P, FRAMES * SEQS * PACK], BF16, align_bytes=64)
         nc.scalar.copy(
-            out=g_grouped[:].bitcast(F32).rearrange("p (t b u) -> p t b u", t=FRAMES, u=HALF),
+            out=g_grouped[:].bitcast(F32).rearrange("p (t b u) -> p t b u", t=FRAMES, u=PAIRS),
             in_=g_turned[:].rearrange("p u (b t) -> p t b u", t=FRAMES),
         )
         g_codes_once = const.tile([P, FRAMES, 1, SEQS], U32, align_bytes=64)
@@ -216,7 +221,7 @@ def tile_st_hmr_pc_kernel(tc, h_new, c_new, g_s, c_g_s, Wg_s, Zg_s, bg_s, out_0,
         )
         nc.vector.tensor_copy(
             out=g_scales[:].bitcast(I32).rearrange("p (t n b) -> p t n b", t=FRAMES, n=BONES),
-            in_=g_scales_once[:].bitcast(I32).to_broadcast([P, FRAMES, BONES, SEQS // 4]),
+            in_=g_scales_once[:].bitcast(I32).to_broadcast([P, FRAMES, BONES, SEQS // SCALES_PER_I32]),
         )
 
         h_grouped = const.tile([P, FRAMES * COLS * PACK], BF16, align_bytes=64)
@@ -226,62 +231,69 @@ def tile_st_hmr_pc_kernel(tc, h_new, c_new, g_s, c_g_s, Wg_s, Zg_s, bg_s, out_0,
         c_turned_sb = const.tile([P, BONES, BLOCKS, P], BF16)
 
         def turn_h():
-            h_words = h_sb[:].bitcast(F32).rearrange("p (n q u) -> p n u q", n=BONES, u=HALF)
-            words = h_grouped[:].bitcast(F32).rearrange("p (t a x u) -> p a t x u", t=FRAMES, a=BONES // 2, u=HALF)
+            h_pairs = h_sb[:].bitcast(F32).rearrange("p (n q u) -> p n u q", n=BONES, u=PAIRS)
+            grouped_pairs = h_grouped[:].bitcast(F32).rearrange(
+                "p (t a x u) -> p a t x u", t=FRAMES, a=BONES // BONES_PER_BANK, u=PAIRS
+            )
             h_turned = []
             for n in range(BONES):
-                if n % 2 == 0:
-                    h_turned.append(psum.tile([P, HALF, 2, P], F32, tag="bank", name="h_turned"))
-                for u in range(HALF):
-                    nc.tensor.transpose(h_turned[n // 2][:, u, n % 2, :], h_words[:, n, u, :], ident_f32[:])
-            for a in range(BONES // 2):
-                nc.scalar.copy(out=words[:, a], in_=h_turned[a][:].rearrange("p u n (b t) -> p t (n b) u", t=FRAMES))
+                if n % BONES_PER_BANK == 0:
+                    h_turned.append(psum.tile([P, PAIRS, BONES_PER_BANK, P], F32, tag="bank", name="h_turned"))
+                for u in range(PAIRS):
+                    nc.tensor.transpose(
+                        h_turned[n // BONES_PER_BANK][:, u, n % BONES_PER_BANK, :], h_pairs[:, n, u, :], ident_f32[:]
+                    )
+            for a in range(BONES // BONES_PER_BANK):
+                nc.scalar.copy(
+                    out=grouped_pairs[:, a], in_=h_turned[a][:].rearrange("p u n (b t) -> p t (n b) u", t=FRAMES)
+                )
 
         def turn_bias():
             bias_turned = psum.tile([P, P], BF16, tag="bank")
             nc.tensor.transpose(bias_turned[:], bias_rows[:], ident_bf16[:])
             nc.scalar.copy(out=bias_sb[:], in_=bias_turned[:, 0 : GATES * FRAMES * BLOCKS])
 
-        def turn_c_on_tensor():
+        def turn_c():
+            c_turned = []
             for n in range(BONES):
-                if n % 2 == 0:
-                    c_turned.append(psum.tile([P, 2, BLOCKS, P], BF16, tag="bank", name="c_turned"))
+                if n % BONES_PER_BANK == 0:
+                    c_turned.append(psum.tile([P, BONES_PER_BANK, BLOCKS, P], BF16, tag="bank", name="c_turned"))
                 for f in range(BLOCKS):
                     nc.tensor.transpose(
-                        c_turned[n // 2][:, n % 2, f, :], c_sb[:, n, f * P : (f + 1) * P], ident_bf16[:]
+                        c_turned[n // BONES_PER_BANK][:, n % BONES_PER_BANK, f, :],
+                        c_sb[:, n, f * P : (f + 1) * P],
+                        ident_bf16[:],
                     )
 
-        def c_out_of_psum():
-            for a in range(BONES // 2):
-                nc.scalar.copy(out=c_turned_sb[:, 2 * a : 2 * a + 2], in_=c_turned[a][:])
+            for a in range(BONES // BONES_PER_BANK):
+                nc.vector.tensor_copy(
+                    out=c_turned_sb[:, BONES_PER_BANK * a : BONES_PER_BANK * (a + 1)], in_=c_turned[a][:]
+                )
 
-        for s in range(AHEAD):
-            regroup(s)
-            if s == LOAD_H_BEHIND:
+        def is_step(s):
+            return 0 <= s < len(steps)
+
+        for s in range(-AHEAD, len(steps) + SUMS_BEHIND):
+            if is_step(s + AHEAD):
+                regroup(s + AHEAD)
+            if s + AHEAD == LOAD_H_BEHIND:
                 turn_h()
                 turn_bias()
-        nc.vector.quantize_mx(out=h_codes[:].bitcast(FP8X4), scales=h_scales[:], in_=h_grouped[:])
-        for s in range(AHEAD - 1):
-            quantise(s)
-
-        for s in range(len(steps) + 1):
-            if s + AHEAD < len(steps):
-                regroup(s + AHEAD)
-            if s >= 1:
-                weigh_by_cell(s - 1)
-            if s + AHEAD - 1 < len(steps):
+            if s + AHEAD == LOAD_H_BEHIND + 1:
+                nc.vector.quantize_mx(out=h_codes[:].bitcast(FP8X4), scales=h_scales[:], in_=h_grouped[:])
+            if is_step(s - 1):
+                weigh_by_c_new(s - 1)
+            if is_step(s + AHEAD - 1):
                 quantise(s + AHEAD - 1)
-            if s < len(steps):
+            if is_step(s):
                 gate_matmuls(s)
-            if s == 0:
-                turn_c_on_tensor()
-            if s >= 1:
-                sum_over_bones(s - 1)
-            if s >= 2:
-                squash(s - 2)
-            if s < len(steps):
+            if s + AHEAD == LOAD_C_BEHIND:
+                turn_c()
+            if is_step(s - SUMS_BEHIND):
+                sum_over_bones(s - SUMS_BEHIND)
+            if is_step(s - SUMS_BEHIND - 1):
+                squash(s - SUMS_BEHIND - 1)
+            if is_step(s):
                 sigmoids(s)
-            if s == 0:
-                c_out_of_psum()
-            if s >= 1:
-                combine(s - 1)
+            if is_step(s - SUMS_BEHIND):
+                combine(s - SUMS_BEHIND)

@@ -61,6 +61,10 @@ def tile_st_hmr_pc_kernel(tc, h_new, c_new, g_s, c_g_s, Wg_s, Zg_s, bg_s, out_0,
         c_sb = const.tile([P, BONES, FEATS], BF16)
         bias_rows = const.tile([P, P], BF16)
         cgs_sb = const.tile([P, FRAMES, P], BF16)
+        warm_in = const.tile([P, 1], F32)
+        warm_out = const.tile([P, 1], F32)
+        nc.vector.memset(warm_in[:], 0.0)
+        nc.scalar.activation(out=warm_out[:], in_=warm_in[:], func=ACT.Sigmoid)
         nc.vector.memset(bias_rows[:], 0.0)
         nc.sync.dma_start(out=g_sb[:], in_=g_s.rearrange("b t k -> (b t) k"))
         raw = []

@@ -15,7 +15,7 @@ ALU = mybir.AluOpType
 P = 128
 PACK = 4
 PAIRS = 2
-RUN = 4
+RUN = 8
 SCALES_PER_I32 = 4
 GROUPS_PER_BANK = 2
 BONES_PER_BANK = 2

@@ -32,7 +32,7 @@ KINDS = 2
 FORGET, INPUT, OUTPUT = 0, 1, 2
 GATE_ORDER = (INPUT, FORGET, OUTPUT)
 
-SCALAR_COLS = 256
+SCALAR_COLS = 224
 
 AHEAD = 3
 SUMS_BEHIND = 2

@@ -32,13 +32,15 @@ KINDS = 2
 FORGET, INPUT, OUTPUT = 0, 1, 2
 GATE_ORDER = (INPUT, FORGET, OUTPUT)
 
-SCALAR_COLS = 224
+SCALAR_COLS = 192
+SCALAR_COLS_OUTPUT = 288
 
 AHEAD = 3
 SUMS_BEHIND = 2
 
-LOAD_H_BEHIND = 1
-LOAD_C_BEHIND = 3
+H_CHUNKS = BONES // BONES_PER_BANK
+H_STEPS = H_CHUNKS // KINDS
+LOAD_C_BEHIND = 4
 
 FLOPS = 2 * GATES * FRAMES * FEATS * FEATS * (COLS + SEQS)
 
@@ -57,7 +59,7 @@ def tile_st_hmr_pc_kernel(tc, h_new, c_new, g_s, c_g_s, Wg_s, Zg_s, bg_s, out_0,
         psum = ctx.enter_context(tc.psum_pool(name="psum", bufs=8))
 
         g_sb = const.tile([P, FEATS], BF16)
-        h_sb = const.tile([P, BONES * FEATS], BF16)
+        h_sb = []
         c_sb = const.tile([P, BONES, FEATS], BF16)
         bias_rows = const.tile([P, P], BF16)
         cgs_sb = const.tile([P, FRAMES, P], BF16)
@@ -72,8 +74,16 @@ def tile_st_hmr_pc_kernel(tc, h_new, c_new, g_s, c_g_s, Wg_s, Zg_s, bg_s, out_0,
             raw.append(raw_pool.tile([P, KINDS, PACK, FEATS], BF16, name="raw_%d" % s))
             for kind, weights in ((W, Wg_s), (Z, Zg_s)):
                 nc.sync.dma_start(out=raw[s][:, kind], in_=weights[gate, t].rearrange("(p j) w -> p j w", j=PACK))
-            if s == LOAD_H_BEHIND:
-                nc.sync.dma_start(out=h_sb[:], in_=h_new.rearrange("b t n k -> (b t) (n k)"))
+                if s < H_STEPS:
+                    a = len(h_sb)
+                    h_sb.append(const.tile([P, BONES_PER_BANK * FEATS], BF16, name="h_sb_%d" % a))
+                    nc.sync.dma_start(
+                        out=h_sb[a][:],
+                        in_=h_new[:, :, BONES_PER_BANK * a : BONES_PER_BANK * (a + 1), :].rearrange(
+                            "b t n k -> (b t) (n k)"
+                        ),
+                    )
+            if s == H_STEPS - 1:
                 nc.sync.dma_start(
                     out=bias_rows[0 : GATES * FRAMES * BLOCKS, :],
                     in_=bg_s.rearrange("g t o (f c) -> (g t o f) c", c=P),
@@ -104,10 +114,15 @@ def tile_st_hmr_pc_kernel(tc, h_new, c_new, g_s, c_g_s, Wg_s, Zg_s, bg_s, out_0,
             grouped[s] = grouped_pool.tile([P, KINDS, FEATS, PACK], BF16, align_bytes=64, name="grouped")
             dst = grouped[s][:].rearrange("p m (v i) j -> p m v j i", i=RUN)
             src = raw[s][:].rearrange("p m j (v i) -> p m v j i", i=RUN)
-            cut = (FEATS - SCALAR_COLS) // RUN
-            nc.vector.tensor_copy(out=dst[:, :, :cut], in_=src[:, :, :cut])
-            for kind in (W, Z):
-                nc.scalar.copy(out=dst[:, kind, cut:], in_=src[:, kind, cut:])
+            cut = (FEATS - (SCALAR_COLS_OUTPUT if steps[s][1] == OUTPUT else SCALAR_COLS)) // RUN
+            if s < H_STEPS:
+                for kind in (W, Z):
+                    nc.vector.tensor_copy(out=dst[:, kind, :cut], in_=src[:, kind, :cut])
+                    nc.scalar.copy(out=dst[:, kind, cut:], in_=src[:, kind, cut:])
+                    turn_h(KINDS * s + kind)
+            else:
+                nc.vector.tensor_copy(out=dst[:, :, :cut], in_=src[:, :, :cut])
+                nc.scalar.copy(out=dst[:, :, cut:], in_=src[:, :, cut:])
 
         def quantise(s):
             codes[s] = code_pool.tile([P, KINDS, FEATS], U32, align_bytes=64, name="codes")
@@ -234,23 +249,14 @@ def tile_st_hmr_pc_kernel(tc, h_new, c_new, g_s, c_g_s, Wg_s, Zg_s, bg_s, out_0,
         bias_sb = const.tile([P, GATES * FRAMES * BLOCKS], F32)
         c_turned_sb = const.tile([P, BONES, BLOCKS, P], BF16)
 
-        def turn_h():
-            h_pairs = h_sb[:].bitcast(F32).rearrange("p (n q u) -> p n u q", n=BONES, u=PAIRS)
-            grouped_pairs = h_grouped[:].bitcast(F32).rearrange(
-                "p (t a x u) -> p a t x u", t=FRAMES, a=BONES // BONES_PER_BANK, u=PAIRS
-            )
-            h_turned = []
-            for n in range(BONES):
-                if n % BONES_PER_BANK == 0:
-                    h_turned.append(psum.tile([P, PAIRS, BONES_PER_BANK, P], F32, tag="bank", name="h_turned"))
+        def turn_h(a):
+            h_pairs = h_sb[a][:].bitcast(F32).rearrange("p (n q u) -> p n u q", n=BONES_PER_BANK, u=PAIRS)
+            grouped_pairs = h_grouped[:].bitcast(F32).rearrange("p (t a x u) -> p a t x u", t=FRAMES, a=H_CHUNKS, u=PAIRS)
+            h_turned = psum.tile([P, PAIRS, BONES_PER_BANK, P], F32, tag="bank", name="h_turned")
+            for n in range(BONES_PER_BANK):
                 for u in range(PAIRS):
-                    nc.tensor.transpose(
-                        h_turned[n // BONES_PER_BANK][:, u, n % BONES_PER_BANK, :], h_pairs[:, n, u, :], ident_f32[:]
-                    )
-            for a in range(BONES // BONES_PER_BANK):
-                nc.scalar.copy(
-                    out=grouped_pairs[:, a], in_=h_turned[a][:].rearrange("p u n (b t) -> p t (n b) u", t=FRAMES)
-                )
+                    nc.tensor.transpose(h_turned[:, u, n, :], h_pairs[:, n, u, :], ident_f32[:])
+            nc.scalar.copy(out=grouped_pairs[:, a], in_=h_turned[:].rearrange("p u n (b t) -> p t (n b) u", t=FRAMES))
 
         def turn_bias():
             bias_turned = psum.tile([P, P], BF16, tag="bank")
@@ -280,10 +286,9 @@ def tile_st_hmr_pc_kernel(tc, h_new, c_new, g_s, c_g_s, Wg_s, Zg_s, bg_s, out_0,
         for s in range(-AHEAD, len(steps) + SUMS_BEHIND):
             if is_step(s + AHEAD):
                 regroup(s + AHEAD)
-            if s + AHEAD == LOAD_H_BEHIND:
-                turn_h()
+            if s + AHEAD == H_STEPS - 1:
                 turn_bias()
-            if s + AHEAD == LOAD_H_BEHIND + 1:
+            if s + AHEAD == H_STEPS:
                 nc.vector.quantize_mx(out=h_codes[:].bitcast(FP8X4), scales=h_scales[:], in_=h_grouped[:])
             if is_step(s - 1):
                 weigh_by_c_new(s - 1)

@@ -284,6 +284,8 @@ def tile_st_hmr_pc_kernel(tc, h_new, c_new, g_s, c_g_s, Wg_s, Zg_s, bg_s, out_0,
             return 0 <= s < len(steps)
 
         for s in range(-AHEAD, len(steps) + SUMS_BEHIND):
+            if s < 0 and is_step(s + AHEAD - 1):
+                quantise(s + AHEAD - 1)
             if is_step(s + AHEAD):
                 regroup(s + AHEAD)
             if s + AHEAD == H_STEPS - 1:
@@ -292,7 +294,7 @@ def tile_st_hmr_pc_kernel(tc, h_new, c_new, g_s, c_g_s, Wg_s, Zg_s, bg_s, out_0,
                 nc.vector.quantize_mx(out=h_codes[:].bitcast(FP8X4), scales=h_scales[:], in_=h_grouped[:])
             if is_step(s - 1):
                 weigh_by_c_new(s - 1)
-            if is_step(s + AHEAD - 1):
+            if s >= 0 and is_step(s + AHEAD - 1):
                 quantise(s + AHEAD - 1)
             if is_step(s):
                 gate_matmuls(s)

@@ -122,7 +122,11 @@ def tile_st_hmr_pc_kernel(tc, h_new, c_new, g_s, c_g_s, Wg_s, Zg_s, bg_s, out_0,
                     turn_h(KINDS * s + kind)
             else:
                 nc.vector.tensor_copy(out=dst[:, :, :cut], in_=src[:, :, :cut])
-                nc.scalar.copy(out=dst[:, :, cut:], in_=src[:, :, cut:])
+                if s <= LOAD_C_BEHIND + 1:
+                    for kind in (W, Z):
+                        nc.scalar.copy(out=dst[:, kind, cut:], in_=src[:, kind, cut:])
+                else:
+                    nc.scalar.copy(out=dst[:, :, cut:], in_=src[:, :, cut:])
 
         def quantise(s):
             codes[s] = code_pool.tile([P, KINDS, FEATS], U32, align_bytes=64, name="codes")

@@ -32,8 +32,10 @@ KINDS = 2
 FORGET, INPUT, OUTPUT = 0, 1, 2
 GATE_ORDER = (INPUT, FORGET, OUTPUT)
 
-SCALAR_COLS = 192
-SCALAR_COLS_OUTPUT = 288
+SCALAR_COLS = 208
+SCALAR_COLS_OUTPUT = 304
+TENSOR_COLS = 72
+TENSOR_FROM = 3
 
 AHEAD = 3
 SUMS_BEHIND = 2
@@ -101,6 +103,7 @@ def tile_st_hmr_pc_kernel(tc, h_new, c_new, g_s, c_g_s, Wg_s, Zg_s, bg_s, out_0,
         make_identity(nc, ident_bf16[:])
 
         grouped = {}
+        side_by_side = {}
         codes = {}
         scales = {}
         acc = {}
@@ -114,19 +117,36 @@ def tile_st_hmr_pc_kernel(tc, h_new, c_new, g_s, c_g_s, Wg_s, Zg_s, bg_s, out_0,
             grouped[s] = grouped_pool.tile([P, KINDS, FEATS, PACK], BF16, align_bytes=64, name="grouped")
             dst = grouped[s][:].rearrange("p m (v i) j -> p m v j i", i=RUN)
             src = raw[s][:].rearrange("p m j (v i) -> p m v j i", i=RUN)
+            end = (FEATS - (TENSOR_COLS if s >= TENSOR_FROM else 0)) // RUN
             cut = (FEATS - (SCALAR_COLS_OUTPUT if steps[s][1] == OUTPUT else SCALAR_COLS)) // RUN
             if s < H_STEPS:
                 for kind in (W, Z):
                     nc.vector.tensor_copy(out=dst[:, kind, :cut], in_=src[:, kind, :cut])
-                    nc.scalar.copy(out=dst[:, kind, cut:], in_=src[:, kind, cut:])
+                    nc.scalar.copy(out=dst[:, kind, cut:end], in_=src[:, kind, cut:end])
                     turn_h(KINDS * s + kind)
             else:
                 nc.vector.tensor_copy(out=dst[:, :, :cut], in_=src[:, :, :cut])
                 if s <= LOAD_C_BEHIND + 1:
                     for kind in (W, Z):
-                        nc.scalar.copy(out=dst[:, kind, cut:], in_=src[:, kind, cut:])
+                        nc.scalar.copy(out=dst[:, kind, cut:end], in_=src[:, kind, cut:end])
                 else:
-                    nc.scalar.copy(out=dst[:, :, cut:], in_=src[:, :, cut:])
+                    nc.scalar.copy(out=dst[:, :, cut:end], in_=src[:, :, cut:end])
+
+        def regroup_on_tensor(s):
+            side_by_side[s] = psum.tile([P, KINDS, TENSOR_COLS * PACK], BF16, tag="bank", name="side_by_side")
+            for kind in (W, Z):
+                nc.tensor.matmul(
+                    out=side_by_side[s][:, kind],
+                    lhsT=ident_bf16[:],
+                    rhs=raw[s][:, kind, :, FEATS - TENSOR_COLS :].rearrange("p j w -> p w j"),
+                    start=True,
+                    stop=True,
+                )
+
+        def take_from_tensor(s):
+            nc.scalar.copy(
+                out=grouped[s][:, :, FEATS - TENSOR_COLS :, :].rearrange("p m w j -> p m (w j)"), in_=side_by_side[s][:]
+            )
 
         def quantise(s):
             codes[s] = code_pool.tile([P, KINDS, FEATS], U32, align_bytes=64, name="codes")
@@ -302,6 +322,8 @@ def tile_st_hmr_pc_kernel(tc, h_new, c_new, g_s, c_g_s, Wg_s, Zg_s, bg_s, out_0,
                 quantise(s + AHEAD - 1)
             if is_step(s):
                 gate_matmuls(s)
+            if is_step(s + AHEAD) and s + AHEAD >= TENSOR_FROM:
+                regroup_on_tensor(s + AHEAD)
             if s + AHEAD == LOAD_C_BEHIND:
                 turn_c()
             if is_step(s - SUMS_BEHIND):
@@ -310,5 +332,7 @@ def tile_st_hmr_pc_kernel(tc, h_new, c_new, g_s, c_g_s, Wg_s, Zg_s, bg_s, out_0,
                 squash(s - SUMS_BEHIND - 1)
             if is_step(s):
                 sigmoids(s)
+            if is_step(s + AHEAD) and s + AHEAD >= TENSOR_FROM:
+                take_from_tensor(s + AHEAD)
             if is_step(s - SUMS_BEHIND):
                 combine(s - SUMS_BEHIND)

@@ -32,10 +32,12 @@ KINDS = 2
 FORGET, INPUT, OUTPUT = 0, 1, 2
 GATE_ORDER = (INPUT, FORGET, OUTPUT)
 
-SCALAR_COLS = 208
+SCALAR_COLS = 200
 SCALAR_COLS_OUTPUT = 304
-TENSOR_COLS = 72
-TENSOR_FROM = 3
+TENSOR_COLS = 80
+TENSOR_MORE = 16
+TENSOR_FROM = 4
+TENSOR_TO = 11
 
 AHEAD = 3
 SUMS_BEHIND = 2
@@ -113,12 +115,16 @@ def tile_st_hmr_pc_kernel(tc, h_new, c_new, g_s, c_g_s, Wg_s, Zg_s, bg_s, out_0,
         cell = {}
         squashed = {}
 
+        def on_tensor(s):
+            return TENSOR_FROM <= s < TENSOR_TO
+
         def regroup(s):
             grouped[s] = grouped_pool.tile([P, KINDS, FEATS, PACK], BF16, align_bytes=64, name="grouped")
             dst = grouped[s][:].rearrange("p m (v i) j -> p m v j i", i=RUN)
             src = raw[s][:].rearrange("p m j (v i) -> p m v j i", i=RUN)
-            end = (FEATS - (TENSOR_COLS if s >= TENSOR_FROM else 0)) // RUN
-            cut = (FEATS - (SCALAR_COLS_OUTPUT if steps[s][1] == OUTPUT else SCALAR_COLS)) // RUN
+            share = SCALAR_COLS_OUTPUT if steps[s][1] == OUTPUT else SCALAR_COLS
+            cut = (FEATS - share - (TENSOR_MORE if on_tensor(s) else 0)) // RUN
+            end = (FEATS - (TENSOR_COLS if on_tensor(s) else 0)) // RUN
             if s < H_STEPS:
                 for kind in (W, Z):
                     nc.vector.tensor_copy(out=dst[:, kind, :cut], in_=src[:, kind, :cut])
@@ -192,9 +198,15 @@ def tile_st_hmr_pc_kernel(tc, h_new, c_new, g_s, c_g_s, Wg_s, Zg_s, bg_s, out_0,
         def weigh_by_c_new(s):
             t, gate = steps[s]
             if gate == FORGET:
-                gate_view = sig[s][:].rearrange("p n f b -> p (n f) b")
-                c_view = c_turned_sb[:].rearrange("p n f (b t) -> p t (n f) b", t=FRAMES)
-                nc.vector.tensor_mul(out=gate_view, in0=gate_view, in1=c_view[:, t])
+                if t < FRAMES - 1:
+                    gate_view = sig[s][:].rearrange("p n f b -> p (n f) b")
+                    c_view = c_turned_sb[:].rearrange("p n f (b t) -> p t (n f) b", t=FRAMES)
+                    nc.vector.tensor_mul(out=gate_view, in0=gate_view, in1=c_view[:, t])
+                else:
+                    for half in (slice(0, 2), slice(2, 4)):
+                        gate_view = sig[s][:, :, half, :]
+                        c_view = c_turned_sb[:, :, half].rearrange("p n f (b t) -> p t n f b", t=FRAMES)
+                        nc.vector.tensor_mul(out=gate_view, in0=gate_view, in1=c_view[:, t])
 
         def sum_over_bones(s):
             red[s] = psum.tile([P, P], F32, tag="bank", name="red")
@@ -322,7 +334,7 @@ def tile_st_hmr_pc_kernel(tc, h_new, c_new, g_s, c_g_s, Wg_s, Zg_s, bg_s, out_0,
                 quantise(s + AHEAD - 1)
             if is_step(s):
                 gate_matmuls(s)
-            if is_step(s + AHEAD) and s + AHEAD >= TENSOR_FROM:
+            if on_tensor(s + AHEAD):
                 regroup_on_tensor(s + AHEAD)
             if s + AHEAD == LOAD_C_BEHIND:
                 turn_c()
@@ -332,7 +344,7 @@ def tile_st_hmr_pc_kernel(tc, h_new, c_new, g_s, c_g_s, Wg_s, Zg_s, bg_s, out_0,
                 squash(s - SUMS_BEHIND - 1)
             if is_step(s):
                 sigmoids(s)
-            if is_step(s + AHEAD) and s + AHEAD >= TENSOR_FROM:
+            if on_tensor(s + AHEAD):
                 take_from_tensor(s + AHEAD)
             if is_step(s - SUMS_BEHIND):
                 combine(s - SUMS_BEHIND)

@@ -33,6 +33,7 @@ FORGET, INPUT, OUTPUT = 0, 1, 2
 GATE_ORDER = (INPUT, FORGET, OUTPUT)
 
 SCALAR_COLS = 200
+SCALAR_COLS_LAST = 256
 SCALAR_COLS_OUTPUT = 304
 TENSOR_COLS = 80
 TENSOR_MORE = 16
@@ -123,6 +124,8 @@ def tile_st_hmr_pc_kernel(tc, h_new, c_new, g_s, c_g_s, Wg_s, Zg_s, bg_s, out_0,
             dst = grouped[s][:].rearrange("p m (v i) j -> p m v j i", i=RUN)
             src = raw[s][:].rearrange("p m j (v i) -> p m v j i", i=RUN)
             share = SCALAR_COLS_OUTPUT if steps[s][1] == OUTPUT else SCALAR_COLS
+            if s == len(steps) - 1:
+                share = SCALAR_COLS_LAST
             cut = (FEATS - share - (TENSOR_MORE if on_tensor(s) else 0)) // RUN
             end = (FEATS - (TENSOR_COLS if on_tensor(s) else 0)) // RUN
             if s < H_STEPS:
@@ -203,9 +206,9 @@ def tile_st_hmr_pc_kernel(tc, h_new, c_new, g_s, c_g_s, Wg_s, Zg_s, bg_s, out_0,
                     c_view = c_turned_sb[:].rearrange("p n f (b t) -> p t (n f) b", t=FRAMES)
                     nc.vector.tensor_mul(out=gate_view, in0=gate_view, in1=c_view[:, t])
                 else:
-                    for half in (slice(0, 2), slice(2, 4)):
-                        gate_view = sig[s][:, :, half, :]
-                        c_view = c_turned_sb[:, :, half].rearrange("p n f (b t) -> p t n f b", t=FRAMES)
+                    for f in range(BLOCKS):
+                        gate_view = sig[s][:, :, f, :]
+                        c_view = c_turned_sb[:, :, f].rearrange("p n (b t) -> p t n b", t=FRAMES)
                         nc.vector.tensor_mul(out=gate_view, in0=gate_view, in1=c_view[:, t])
 
         def sum_over_bones(s):
@@ -322,7 +325,7 @@ def tile_st_hmr_pc_kernel(tc, h_new, c_new, g_s, c_g_s, Wg_s, Zg_s, bg_s, out_0,
         for s in range(-AHEAD, len(steps) + SUMS_BEHIND):
             if s < 0 and is_step(s + AHEAD - 1):
                 quantise(s + AHEAD - 1)
-            if is_step(s + AHEAD):
+            if is_step(s + AHEAD) and s + AHEAD < len(steps) - 1:
                 regroup(s + AHEAD)
             if s + AHEAD == H_STEPS - 1:
                 turn_bias()
@@ -332,6 +335,8 @@ def tile_st_hmr_pc_kernel(tc, h_new, c_new, g_s, c_g_s, Wg_s, Zg_s, bg_s, out_0,
                 weigh_by_c_new(s - 1)
             if s >= 0 and is_step(s + AHEAD - 1):
                 quantise(s + AHEAD - 1)
+            if s + AHEAD == len(steps) - 1:
+                regroup(s + AHEAD)
             if is_step(s):
                 gate_matmuls(s)
             if on_tensor(s + AHEAD):

@@ -46,6 +46,7 @@ SUMS_BEHIND = 2
 H_CHUNKS = BONES // BONES_PER_BANK
 H_STEPS = H_CHUNKS // KINDS
 LOAD_C_BEHIND = 4
+LOAD_CGS_BEHIND = 6
 
 FLOPS = 2 * GATES * FRAMES * FEATS * FEATS * (COLS + SEQS)
 
@@ -95,6 +96,7 @@ def tile_st_hmr_pc_kernel(tc, h_new, c_new, g_s, c_g_s, Wg_s, Zg_s, bg_s, out_0,
                 )
             if s == LOAD_C_BEHIND:
                 nc.sync.dma_start(out=c_sb[:], in_=c_new.rearrange("b t n k -> (b t) n k"))
+            if s == LOAD_CGS_BEHIND:
                 for f in range(BLOCKS):
                     nc.sync.dma_start(
                         out=cgs_sb[f * SEQS : (f + 1) * SEQS, :, :], in_=c_g_s[:, :, f * P : (f + 1) * P]
@@ -351,5 +353,7 @@ def tile_st_hmr_pc_kernel(tc, h_new, c_new, g_s, c_g_s, Wg_s, Zg_s, bg_s, out_0,
                 sigmoids(s)
             if on_tensor(s + AHEAD):
                 take_from_tensor(s + AHEAD)
-            if is_step(s - SUMS_BEHIND):
+            if s - SUMS_BEHIND == 1:
+                combine(0)
+            if is_step(s - SUMS_BEHIND) and s > SUMS_BEHIND:
                 combine(s - SUMS_BEHIND)

@@ -146,13 +146,15 @@ def tile_st_hmr_pc_kernel(tc, h_new, c_new, g_s, c_g_s, Wg_s, Zg_s, bg_s, out_0,
         def regroup_on_tensor(s):
             side_by_side[s] = psum.tile([P, KINDS, TENSOR_COLS * PACK], BF16, tag="bank", name="side_by_side")
             for kind in (W, Z):
-                nc.tensor.matmul(
-                    out=side_by_side[s][:, kind],
-                    lhsT=ident_bf16[:],
-                    rhs=raw[s][:, kind, :, FEATS - TENSOR_COLS :].rearrange("p j w -> p w j"),
-                    start=True,
-                    stop=True,
-                )
+                pairs = side_by_side[s][:, kind].rearrange("p (w u e) -> p u w e", u=PAIRS, e=PACK // PAIRS)
+                for u in range(PAIRS):
+                    nc.tensor.matmul(
+                        out=pairs[:, u],
+                        lhsT=ident_bf16[:],
+                        rhs=raw[s][:, kind, PAIRS * u : PAIRS * (u + 1), FEATS - TENSOR_COLS :].rearrange("p e w -> p w e"),
+                        start=True,
+                        stop=True,
+                    )
 
         def take_from_tensor(s):
             nc.scalar.copy(
@@ -335,7 +337,7 @@ def tile_st_hmr_pc_kernel(tc, h_new, c_new, g_s, c_g_s, Wg_s, Zg_s, bg_s, out_0,
                 nc.vector.quantize_mx(out=h_codes[:].bitcast(FP8X4), scales=h_scales[:], in_=h_grouped[:])
             if is_step(s - 1):
                 weigh_by_c_new(s - 1)
-            if s >= 0 and is_step(s + AHEAD - 1):
+            if s >= 0 and s + AHEAD < len(steps):
                 quantise(s + AHEAD - 1)
             if s + AHEAD == len(steps) - 1:
                 regroup(s + AHEAD)
@@ -347,6 +349,9 @@ def tile_st_hmr_pc_kernel(tc, h_new, c_new, g_s, c_g_s, Wg_s, Zg_s, bg_s, out_0,
                 turn_c()
             if is_step(s - SUMS_BEHIND):
                 sum_over_bones(s - SUMS_BEHIND)
+            if s + AHEAD == len(steps):
+                combine(s - SUMS_BEHIND)
+                quantise(s + AHEAD - 1)
             if is_step(s - SUMS_BEHIND - 1):
                 squash(s - SUMS_BEHIND - 1)
             if is_step(s):
@@ -355,5 +360,5 @@ def tile_st_hmr_pc_kernel(tc, h_new, c_new, g_s, c_g_s, Wg_s, Zg_s, bg_s, out_0,
                 take_from_tensor(s + AHEAD)
             if s - SUMS_BEHIND == 1:
                 combine(0)
-            if is_step(s - SUMS_BEHIND) and s > SUMS_BEHIND:
+            if is_step(s - SUMS_BEHIND) and s > SUMS_BEHIND and s + AHEAD != len(steps):
                 combine(s - SUMS_BEHIND)

from contextlib import ExitStack

import concourse.mybir as mybir
from concourse.masks import make_identity

BF16 = mybir.dt.bfloat16
F32 = mybir.dt.float32
I32 = mybir.dt.int32
U32 = mybir.dt.uint32
U8 = mybir.dt.uint8
FP8X4 = mybir.dt.float8_e4m3fn_x4
ACT = mybir.ActivationFunctionType
ALU = mybir.AluOpType

P = 128
PACK = 4
PAIRS = 2
RUN = 8
SCALES_PER_I32 = 4
GROUPS_PER_BANK = 2
BONES_PER_BANK = 2
SEQS = 32
FRAMES = 4
BONES = 8
FEATS = 512
GATES = 3
BLOCKS = FEATS // P
COLS = BONES * SEQS
W, Z = 0, 1
KINDS = 2

FORGET, INPUT, OUTPUT = 0, 1, 2
GATE_ORDER = (INPUT, FORGET, OUTPUT)

SCALAR_COLS = 200
SCALAR_COLS_LAST = 256
SCALAR_COLS_OUTPUT = 304
TENSOR_COLS = 80
TENSOR_MORE = 16
TENSOR_FROM = 4
TENSOR_TO = 11

AHEAD = 3
SUMS_BEHIND = 2

H_CHUNKS = BONES // BONES_PER_BANK
H_STEPS = H_CHUNKS // KINDS
LOAD_C_BEHIND = 4
LOAD_CGS_BEHIND = 6

FLOPS = 2 * GATES * FRAMES * FEATS * FEATS * (COLS + SEQS)


def tile_st_hmr_pc_kernel(tc, h_new, c_new, g_s, c_g_s, Wg_s, Zg_s, bg_s, out_0, out_1):
    nc = tc.nc
    steps = [(t, gate) for t in range(FRAMES) for gate in GATE_ORDER]
    with ExitStack() as ctx:
        ctx.enter_context(tc.manual_schedule())
        const = ctx.enter_context(tc.tile_pool(name="const", bufs=1))
        raw_pool = ctx.enter_context(tc.tile_pool(name="raw", bufs=1))
        grouped_pool = ctx.enter_context(tc.tile_pool(name="grouped", bufs=3))
        code_pool = ctx.enter_context(tc.tile_pool(name="codes", bufs=AHEAD + 1))
        sig_pool = ctx.enter_context(tc.tile_pool(name="sig", bufs=SUMS_BEHIND + 2))
        fin_pool = ctx.enter_context(tc.tile_pool(name="fin", bufs=FRAMES))
        psum = ctx.enter_context(tc.psum_pool(name="psum", bufs=8))

        g_sb = const.tile([P, FEATS], BF16)
        h_sb = []
        c_sb = const.tile([P, BONES, FEATS], BF16)
        bias_rows = const.tile([P, P], BF16)
        cgs_sb = const.tile([P, FRAMES, P], BF16)
        warm_in = const.tile([P, 1], F32)
        warm_out = const.tile([P, 1], F32)
        nc.vector.memset(warm_in[:], 0.0)
        nc.scalar.activation(out=warm_out[:], in_=warm_in[:], func=ACT.Sigmoid)
        nc.vector.memset(bias_rows[:], 0.0)
        nc.sync.dma_start(out=g_sb[:], in_=g_s.rearrange("b t k -> (b t) k"))
        raw = []
        for s, (t, gate) in enumerate(steps):
            raw.append(raw_pool.tile([P, KINDS, PACK, FEATS], BF16, name="raw_%d" % s))
            for kind, weights in ((W, Wg_s), (Z, Zg_s)):
                nc.sync.dma_start(out=raw[s][:, kind], in_=weights[gate, t].rearrange("(p j) w -> p j w", j=PACK))
                if s < H_STEPS:
                    a = len(h_sb)
                    h_sb.append(const.tile([P, BONES_PER_BANK * FEATS], BF16, name="h_sb_%d" % a))
                    nc.sync.dma_start(
                        out=h_sb[a][:],
                        in_=h_new[:, :, BONES_PER_BANK * a : BONES_PER_BANK * (a + 1), :].rearrange(
                            "b t n k -> (b t) (n k)"
                        ),
                    )
            if s == H_STEPS - 1:
                nc.sync.dma_start(
                    out=bias_rows[0 : GATES * FRAMES * BLOCKS, :],
                    in_=bg_s.rearrange("g t o (f c) -> (g t o f) c", c=P),
                )
            if s == LOAD_C_BEHIND:
                nc.sync.dma_start(out=c_sb[:], in_=c_new.rearrange("b t n k -> (b t) n k"))
            if s == LOAD_CGS_BEHIND:
                for f in range(BLOCKS):
                    nc.sync.dma_start(
                        out=cgs_sb[f * SEQS : (f + 1) * SEQS, :, :], in_=c_g_s[:, :, f * P : (f + 1) * P]
                    )

        ident_f32 = const.tile([P, P], F32)
        make_identity(nc, ident_f32[:])
        ident_bf16 = const.tile([P, P], BF16)
        make_identity(nc, ident_bf16[:])

        grouped = {}
        side_by_side = {}
        codes = {}
        scales = {}
        acc = {}
        sig = {}
        red = {}
        kept = {}
        cell = {}
        squashed = {}

        def on_tensor(s):
            return TENSOR_FROM <= s < TENSOR_TO

        def regroup(s):
            grouped[s] = grouped_pool.tile([P, KINDS, FEATS, PACK], BF16, align_bytes=64, name="grouped")
            dst = grouped[s][:].rearrange("p m (v i) j -> p m v j i", i=RUN)
            src = raw[s][:].rearrange("p m j (v i) -> p m v j i", i=RUN)
            share = SCALAR_COLS_OUTPUT if steps[s][1] == OUTPUT else SCALAR_COLS
            if s == len(steps) - 1:
                share = SCALAR_COLS_LAST
            cut = (FEATS - share - (TENSOR_MORE if on_tensor(s) else 0)) // RUN
            end = (FEATS - (TENSOR_COLS if on_tensor(s) else 0)) // RUN
            if s < H_STEPS:
                for kind in (W, Z):
                    nc.vector.tensor_copy(out=dst[:, kind, :cut], in_=src[:, kind, :cut])
                    nc.scalar.copy(out=dst[:, kind, cut:end], in_=src[:, kind, cut:end])
                    turn_h(KINDS * s + kind)
            else:
                nc.vector.tensor_copy(out=dst[:, :, :cut], in_=src[:, :, :cut])
                if s <= LOAD_C_BEHIND + 1:
                    for kind in (W, Z):
                        nc.scalar.copy(out=dst[:, kind, cut:end], in_=src[:, kind, cut:end])
                else:
                    nc.scalar.copy(out=dst[:, :, cut:end], in_=src[:, :, cut:end])

        def regroup_on_tensor(s):
            side_by_side[s] = psum.tile([P, KINDS, TENSOR_COLS * PACK], BF16, tag="bank", name="side_by_side")
            for kind in (W, Z):
                pairs = side_by_side[s][:, kind].rearrange("p (w u e) -> p u w e", u=PAIRS, e=PACK // PAIRS)
                for u in range(PAIRS):
                    nc.tensor.matmul(
                        out=pairs[:, u],
                        lhsT=ident_bf16[:],
                        rhs=raw[s][:, kind, PAIRS * u : PAIRS * (u + 1), FEATS - TENSOR_COLS :].rearrange("p e w -> p w e"),
                        start=True,
                        stop=True,
                    )

        def take_from_tensor(s):
            nc.scalar.copy(
                out=grouped[s][:, :, FEATS - TENSOR_COLS :, :].rearrange("p m w j -> p m (w j)"), in_=side_by_side[s][:]
            )

        def quantise(s):
            codes[s] = code_pool.tile([P, KINDS, FEATS], U32, align_bytes=64, name="codes")
            scales[s] = code_pool.tile([P, KINDS, FEATS], U8, align_bytes=64, name="scales")
            nc.vector.quantize_mx(
                out=codes[s][:].rearrange("p m w -> p (m w)").bitcast(FP8X4),
                scales=scales[s][:].rearrange("p m w -> p (m w)"),
                in_=grouped[s][:].rearrange("p m w j -> p (m w j)"),
            )

        def gate_matmuls(s):
            t = steps[s][0]
            frame_cols = slice(t * COLS, (t + 1) * COLS)
            moving = {W: (h_codes, h_scales), Z: (g_codes, g_scales)}
            acc[s] = []
            for f in range(BLOCKS):
                if f % GROUPS_PER_BANK == 0:
                    acc[s].append(psum.tile([P, GROUPS_PER_BANK, COLS], F32, tag="bank", name="acc"))
                block_cols = slice(f * P, (f + 1) * P)
                for kind in (W, Z):
                    nc.tensor.matmul_mx(
                        out=acc[s][f // GROUPS_PER_BANK][:, f % GROUPS_PER_BANK, :],
                        lhsT=codes[s][:, kind, block_cols].bitcast(FP8X4),
                        lhsT_scale=scales[s][:, kind, block_cols],
                        rhs=moving[kind][0][:, frame_cols].bitcast(FP8X4),
                        rhs_scale=moving[kind][1][:, frame_cols],
                        start=(kind == W),
                        stop=(kind == Z),
                    )

        def sigmoids(s):
            t, gate = steps[s]
            sig[s] = sig_pool.tile([P, BONES, BLOCKS, SEQS], F32, name="sig")
            for f in range(BLOCKS):
                bias_col = (gate * FRAMES + t) * BLOCKS + f
                nc.scalar.activation(
                    out=sig[s][:, :, f, :],
                    in_=acc[s][f // GROUPS_PER_BANK][:, f % GROUPS_PER_BANK, :].rearrange("p (n b) -> p n b", b=SEQS),
                    func=ACT.Sigmoid,
                    bias=bias_sb[:, bias_col : bias_col + 1],
                )

        def weigh_by_c_new(s):
            t, gate = steps[s]
            if gate == FORGET:
                if t < FRAMES - 1:
                    gate_view = sig[s][:].rearrange("p n f b -> p (n f) b")
                    c_view = c_turned_sb[:].rearrange("p n f (b t) -> p t (n f) b", t=FRAMES)
                    nc.vector.tensor_mul(out=gate_view, in0=gate_view, in1=c_view[:, t])
                else:
                    for f in range(BLOCKS):
                        gate_view = sig[s][:, :, f, :]
                        c_view = c_turned_sb[:, :, f].rearrange("p n (b t) -> p t n b", t=FRAMES)
                        nc.vector.tensor_mul(out=gate_view, in0=gate_view, in1=c_view[:, t])

        def sum_over_bones(s):
            red[s] = psum.tile([P, P], F32, tag="bank", name="red")
            for n in range(BONES):
                nc.tensor.matmul(
                    out=red[s][:],
                    lhsT=sig[s][:, n].rearrange("p f b -> p (f b)"),
                    rhs=ident_f32[:],
                    is_transpose=True,
                    start=(n == 0),
                    stop=(n == BONES - 1),
                )

        def store(out, t, result):
            for f in range(BLOCKS):
                nc.sync.dma_start(out=out[:, t, f * P : (f + 1) * P], in_=result[f * SEQS : (f + 1) * SEQS, :])

        def combine(s):
            t, gate = steps[s]
            mean = 1.0 / BONES
            if gate == INPUT:
                kept[t] = fin_pool.tile([P, P], F32, name="kept")
                nc.vector.scalar_tensor_tensor(
                    out=kept[t][:], in0=red[s][:], scalar=mean, in1=cgs_sb[:, t, :], op0=ALU.mult, op1=ALU.mult
                )
            if gate == FORGET:
                cell[t] = fin_pool.tile([P, P], F32, name="cell")
                nc.vector.scalar_tensor_tensor(
                    out=cell[t][:], in0=red[s][:], scalar=mean, in1=kept[t][:], op0=ALU.mult, op1=ALU.add
                )
                store(out_1, t, cell[t])
            if gate == OUTPUT:
                hidden = fin_pool.tile([P, P], F32, name="hidden")
                nc.vector.scalar_tensor_tensor(
                    out=hidden[:], in0=red[s][:], scalar=mean, in1=squashed[t][:], op0=ALU.mult, op1=ALU.mult
                )
                store(out_0, t, hidden)

        def squash(s):
            t, gate = steps[s]
            if gate == FORGET:
                squashed[t] = fin_pool.tile([P, P], F32, name="squashed")
                nc.scalar.activation(out=squashed[t][:], in_=cell[t][:], func=ACT.Tanh)

        g_pairs = g_sb[:].bitcast(F32).rearrange("p (q u) -> p u q", u=PAIRS)
        g_turned = psum.tile([P, PAIRS, P], F32, tag="bank")
        for u in range(PAIRS):
            nc.tensor.transpose(g_turned[:, u, :], g_pairs[:, u, :], ident_f32[:])
        g_grouped = const.tile([P, FRAMES * SEQS * PACK], BF16, align_bytes=64)
        nc.scalar.copy(
            out=g_grouped[:].bitcast(F32).rearrange("p (t b u) -> p t b u", t=FRAMES, u=PAIRS),
            in_=g_turned[:].rearrange("p u (b t) -> p t b u", t=FRAMES),
        )
        g_codes_once = const.tile([P, FRAMES, 1, SEQS], U32, align_bytes=64)
        g_scales_once = const.tile([P, FRAMES, 1, SEQS], U8, align_bytes=64)
        nc.vector.memset(g_scales_once[:].bitcast(I32), 0)
        nc.vector.quantize_mx(
            out=g_codes_once[:].rearrange("p t o b -> p (t o b)").bitcast(FP8X4),
            scales=g_scales_once[:].rearrange("p t o b -> p (t o b)"),
            in_=g_grouped[:],
        )
        g_codes = const.tile([P, FRAMES * COLS], U32, align_bytes=64)
        g_scales = const.tile([P, FRAMES * COLS], U8, align_bytes=64)
        nc.vector.tensor_copy(
            out=g_codes[:].bitcast(I32).rearrange("p (t n b) -> p t n b", t=FRAMES, n=BONES),
            in_=g_codes_once[:].bitcast(I32).to_broadcast([P, FRAMES, BONES, SEQS]),
        )
        nc.vector.tensor_copy(
            out=g_scales[:].bitcast(I32).rearrange("p (t n b) -> p t n b", t=FRAMES, n=BONES),
            in_=g_scales_once[:].bitcast(I32).to_broadcast([P, FRAMES, BONES, SEQS // SCALES_PER_I32]),
        )

        h_grouped = const.tile([P, FRAMES * COLS * PACK], BF16, align_bytes=64)
        h_codes = const.tile([P, FRAMES * COLS], U32, align_bytes=64)
        h_scales = const.tile([P, FRAMES * COLS], U8, align_bytes=64)
        bias_sb = const.tile([P, GATES * FRAMES * BLOCKS], F32)
        c_turned_sb = const.tile([P, BONES, BLOCKS, P], BF16)

        def turn_h(a):
            h_pairs = h_sb[a][:].bitcast(F32).rearrange("p (n q u) -> p n u q", n=BONES_PER_BANK, u=PAIRS)
            grouped_pairs = h_grouped[:].bitcast(F32).rearrange("p (t a x u) -> p a t x u", t=FRAMES, a=H_CHUNKS, u=PAIRS)
            h_turned = psum.tile([P, PAIRS, BONES_PER_BANK, P], F32, tag="bank", name="h_turned")
            for n in range(BONES_PER_BANK):
                for u in range(PAIRS):
                    nc.tensor.transpose(h_turned[:, u, n, :], h_pairs[:, n, u, :], ident_f32[:])
            nc.scalar.copy(out=grouped_pairs[:, a], in_=h_turned[:].rearrange("p u n (b t) -> p t (n b) u", t=FRAMES))

        def turn_bias():
            bias_turned = psum.tile([P, P], BF16, tag="bank")
            nc.tensor.transpose(bias_turned[:], bias_rows[:], ident_bf16[:])
            nc.scalar.copy(out=bias_sb[:], in_=bias_turned[:, 0 : GATES * FRAMES * BLOCKS])

        def turn_c():
            c_turned = []
            for n in range(BONES):
                if n % BONES_PER_BANK == 0:
                    c_turned.append(psum.tile([P, BONES_PER_BANK, BLOCKS, P], BF16, tag="bank", name="c_turned"))
                for f in range(BLOCKS):
                    nc.tensor.transpose(
                        c_turned[n // BONES_PER_BANK][:, n % BONES_PER_BANK, f, :],
                        c_sb[:, n, f * P : (f + 1) * P],
                        ident_bf16[:],
                    )

            for a in range(BONES // BONES_PER_BANK):
                nc.vector.tensor_copy(
                    out=c_turned_sb[:, BONES_PER_BANK * a : BONES_PER_BANK * (a + 1)], in_=c_turned[a][:]
                )

        def is_step(s):
            return 0 <= s < len(steps)

        for s in range(-AHEAD, len(steps) + SUMS_BEHIND):
            if s < 0 and is_step(s + AHEAD - 1):
                quantise(s + AHEAD - 1)
            if is_step(s + AHEAD) and s + AHEAD < len(steps) - 1:
                regroup(s + AHEAD)
            if s + AHEAD == H_STEPS - 1:
                turn_bias()
            if s + AHEAD == H_STEPS:
                nc.vector.quantize_mx(out=h_codes[:].bitcast(FP8X4), scales=h_scales[:], in_=h_grouped[:])
            if is_step(s - 1):
                weigh_by_c_new(s - 1)
            if s >= 0 and s + AHEAD < len(steps):
                quantise(s + AHEAD - 1)
            if s + AHEAD == len(steps) - 1:
                regroup(s + AHEAD)
            if is_step(s):
                gate_matmuls(s)
            if on_tensor(s + AHEAD):
                regroup_on_tensor(s + AHEAD)
            if s + AHEAD == LOAD_C_BEHIND:
                turn_c()
            if is_step(s - SUMS_BEHIND):
                sum_over_bones(s - SUMS_BEHIND)
            if s + AHEAD == len(steps):
                combine(s - SUMS_BEHIND)
                quantise(s + AHEAD - 1)
            if is_step(s - SUMS_BEHIND - 1):
                squash(s - SUMS_BEHIND - 1)
            if is_step(s):
                sigmoids(s)
            if on_tensor(s + AHEAD):
                take_from_tensor(s + AHEAD)
            if s - SUMS_BEHIND == 1:
                combine(0)
            if is_step(s - SUMS_BEHIND) and s > SUMS_BEHIND and s + AHEAD != len(steps):
                combine(s - SUMS_BEHIND)
